import numpy as np
import ml_dtypes


def mxq(x, axis, fmt="e4m3"):
    dtype, down = {"e4m3": (ml_dtypes.float8_e4m3fn, 7), "e5m2": (ml_dtypes.float8_e5m2, 14)}[fmt]
    v = np.moveaxis(np.asarray(x, np.float32).astype(ml_dtypes.bfloat16).astype(np.float64), axis, -1)
    blocks = v.reshape(v.shape[:-1] + (-1, 32))
    amax = np.abs(blocks).max(-1, keepdims=True)
    byte = np.maximum(np.where(amax > 0, np.frexp(amax)[1] - 1 + 127, 0) - down, 1)
    scale = np.exp2(byte - 127.0)
    codes = (blocks / scale).astype(np.float32).astype(dtype).astype(np.float64)
    return np.moveaxis((codes * scale).reshape(v.shape), -1, axis)


WIDE = False


def mx_kscale(k):
    if not WIDE:
        return np.ones(k)
    levels = np.array([10, -10, 5, -5, 0])
    a = np.random.permutation(np.resize(levels, k // 512 * 4)).reshape(k // 512, 4)
    idx = np.arange(k)
    return np.exp2(a[idx // 512, idx % 128 // 32])


BF16 = ml_dtypes.bfloat16


def bf(x):
    return np.asarray(x, np.float32).astype(BF16)


def f64(x):
    return np.asarray(x).astype(np.float64)


E2M1 = np.array([0.0, 0.5, 1.0, 1.5, 2.0, 3.0, 4.0, 6.0, -0.0, -0.5, -1.0, -1.5, -2.0, -3.0, -4.0, -6.0])


def pack_weight(w, fmt):
    k, n = w.shape
    w = f64(bf(w)).reshape(k // 32, 32, n)
    amax = np.abs(w).max(1)
    if fmt == "e4m3":
        byte = np.frexp(amax)[1] - 1 + 127 - 7
    else:
        mant, ex = np.frexp(amax / 6.0)
        byte = np.where(mant > 0.5, ex, ex - 1) + 127
    byte = np.clip(np.where(amax > 0, byte, 1), 1, 254)
    scaled = (w * np.exp2(127.0 - byte)[:, None, :]).reshape(k, n).astype(np.float32)
    by_word = np.ascontiguousarray(scaled.reshape(k // 512, 128, 4, n).transpose(0, 1, 3, 2))
    if fmt == "e4m3":
        words = by_word.astype(ml_dtypes.float8_e4m3fn).view(np.uint8)
    else:
        c = by_word.astype(ml_dtypes.float4_e2m1fn).view(np.uint8) & 0xF
        words = c[..., 0::2] | (c[..., 1::2] << 4)
    return np.ascontiguousarray(words), np.ascontiguousarray(byte.astype(np.uint8).reshape(k // 512, 16, n))


def unpack_weight(words, scales, fmt):
    g, p, n, _ = words.shape
    if fmt == "e4m3":
        vals = np.ascontiguousarray(words).view(ml_dtypes.float8_e4m3fn).astype(np.float64)
    else:
        nib = np.empty((g, p, n, 4), np.uint8)
        nib[..., 0::2] = words & 0xF
        nib[..., 1::2] = words >> 4
        vals = E2M1[nib]
    vals = vals * np.repeat(np.exp2(scales.astype(np.float64) - 127.0), 8, axis=1)[..., None]
    return vals.transpose(0, 1, 3, 2).reshape(g * 512, n)


N, D, DO, R0, R1, R2, R3, R4 = 10240, 512, 128, 1, 2, 4, 10, 25
SCALES = (R0, R1, R2, R3)
NS = len(SCALES)
FMT = "e4m3"


def setup_inputs():
    s = mx_kscale(D)
    x = bf(np.random.standard_normal((N, D)) * s)
    stack = np.random.standard_normal((NS, DO, D)) / np.sqrt(D) / s
    cat = np.ascontiguousarray(stack.swapaxes(1, 2)).reshape(-1, DO)
    words, scales = pack_weight(cat, FMT)
    bs = bf(np.random.standard_normal((NS, DO)) * 0.5)
    return {"inputs_c_e": x,
            "Ws_words": words,
            "Ws_scales": scales,
            "bs": bs}


def reference(inputs_c_e, Ws_words, Ws_scales, bs):
    x, b = f64(inputs_c_e), f64(bs)
    Wt = unpack_weight(Ws_words, Ws_scales, FMT).reshape(NS, D, DO)
    outs = []
    for i, r in enumerate(SCALES):
        groups = N // r
        sums = x.reshape(groups, r, D).sum(axis=1)
        h = np.maximum((mxq(sums, 1, "e4m3") @ Wt[i]) + b[i], 0.0) / r
        outs.append(np.repeat(h, r, axis=0))
    return np.concatenate(outs, axis=0)

@@ -1,0 +1,225 @@
+import concourse.mybir as mybir
+from concourse.masks import make_identity
+
+F32 = mybir.dt.float32
+BF16 = mybir.dt.bfloat16
+I32 = mybir.dt.int32
+U32 = mybir.dt.uint32
+U8 = mybir.dt.uint8
+FP8X4 = mybir.dt.float8_e4m3fn_x4
+ADD = mybir.AluOpType.add
+RELU = mybir.ActivationFunctionType.Relu
+
+P = 128
+N = 10240
+D = 512
+DO = 128
+GROUP = (1, 2, 4, 10)
+NS = len(GROUP)
+SLOTS = N // P
+UNIT = 4
+UNITS = SLOTS // UNIT
+BLOCK_UNITS = 5
+BLOCKS = UNITS // BLOCK_UNITS
+PAIR = 2
+
+OPERAND_SCALE = (0, 0, 0, 0, 1, 1, 2)
+OPERANDS = len(OPERAND_SCALE)
+FIRST_OPERAND = (0, 4, 6)
+BANK_PASSES = 4
+
+COPIES = (1, 2, 2, 2)
+
+LOADS_AHEAD = 8
+FLOPS = 2 * D * DO * sum(N // r for r in GROUP)
+
+
+def tile_contractexpand_pa_t_e_kernel(tc, inputs_c_e, Ws_words, Ws_scales, bs, out):
+    nc = tc.nc
+    x_slots = inputs_c_e.rearrange("(p t) k -> p t k", p=P)
+    out_slots = out.rearrange("(s p t) d -> s p t d", s=NS, p=P)
+
+    with tc.tile_pool(name="const", bufs=1) as const, \
+            tc.tile_pool(name="xin", bufs=LOADS_AHEAD + 2) as xin, \
+            tc.tile_pool(name="bf", bufs=5) as bf, \
+            tc.tile_pool(name="sums", bufs=5) as sums, \
+            tc.tile_pool(name="blocksums", bufs=2) as blocksums, \
+            tc.tile_pool(name="mx", bufs=5) as mx, \
+            tc.tile_pool(name="pre", bufs=3) as pre, \
+            tc.tile_pool(name="res", bufs=3) as res, \
+            tc.psum_pool(name="tps", bufs=4) as tps, \
+            tc.psum_pool(name="mps", bufs=4) as mps, \
+            tc.manual_schedule():
+
+        x_nat, to_quantise, codes, scales = {}, {}, {}, {}
+        sum2, sum4, ten_bf, ten_codes, ten_scales = {}, {}, {}, {}, {}
+        biased, ten_biased, results = {}, {}, {}
+
+        def load(n):
+            x_nat[n] = xin.tile([P, UNIT, D], BF16, name="x_nat")
+            nc.sync.dma_start(out=x_nat[n][:], in_=x_slots[:, UNIT * n:UNIT * (n + 1), :])
+
+        def quantise(values, words, plane):
+            nc.vector.quantize_mx(
+                out=words.rearrange("p a c -> p (a c)").bitcast(FP8X4),
+                scales=plane.rearrange("p a c -> p (a c)"),
+                in_=values.rearrange("p a c -> p (a c)"),
+            )
+
+        def product(acc, words, plane, scale):
+            nc.tensor.matmul_mx(
+                out=acc,
+                lhsT=words.bitcast(FP8X4),
+                lhsT_scale=plane,
+                rhs=w_codes[:, scale, :].bitcast(FP8X4),
+                rhs_scale=w_scales[:, scale, :],
+                start=True,
+                stop=True,
+            )
+
+        def relu_and_repeat(scale, values, target):
+            groups = values.shape[1]
+            nc.scalar.activation(
+                out=target,
+                in_=values.unsqueeze(2).to_broadcast([P, groups, COPIES[scale], DO]),
+                func=RELU,
+                scale=1.0 / GROUP[scale],
+            )
+
+        def store(scale, first_slot, tile_):
+            r, c = GROUP[scale], COPIES[scale]
+            slots = tile_.shape[1] * r
+            rows = out_slots[scale][:, first_slot:first_slot + slots, :].rearrange(
+                "p (g k c) d -> p g k (c d)", k=r // c, c=c)
+            for k in range(r // c):
+                nc.sync.dma_start(out=rows[:, :, k, :], in_=tile_.rearrange("p g c d -> p g (c d)"))
+
+        def transpose(n):
+            to_quantise[n] = bf.tile([P, OPERANDS, D], BF16, name="to_quantise", align_bytes=64)
+            for half in range(UNIT // 2):
+                xt = tps.tile([P, 2, 2, P], F32, name="xt")
+                for t in range(2):
+                    words = x_nat[n][:, 2 * half + t, :].bitcast(F32)
+                    for u in range(2):
+                        nc.tensor.transpose(xt[:, t, u, :], words[:, u:D // 2:2], ident[:])
+                nc.scalar.copy(
+                    out=to_quantise[n][:, 2 * half:2 * half + 2, :].bitcast(F32).rearrange(
+                        "p t (r u) -> p t r u", u=2),
+                    in_=xt[:].rearrange("p t u r -> p t r u"),
+                )
+
+        def quantise_x(n):
+            codes[n] = mx.tile([P, OPERANDS, P], U32, name="codes", align_bytes=64)
+            scales[n] = mx.tile([P, OPERANDS, P], U8, name="scales", align_bytes=64)
+            quantise(to_quantise[n][:, 0:4, :], codes[n][:, 0:4, :], scales[n][:, 0:4, :])
+
+        def add_rows(n):
+            block, place = divmod(n, BLOCK_UNITS)
+            sum2[n] = sums.tile([P, 2, D], F32, name="sum2")
+            nc.vector.tensor_tensor(out=sum2[n][:], in0=to_quantise[n][:, 0:4:2, :],
+                                    in1=to_quantise[n][:, 1:4:2, :], op=ADD)
+            if place == 0:
+                sum4[block] = blocksums.tile([P, BLOCK_UNITS, D], F32, name="sum4")
+            nc.vector.tensor_tensor(out=sum4[block][:, place, :], in0=sum2[n][:, 0, :],
+                                    in1=sum2[n][:, 1, :], op=ADD)
+            if place == BLOCK_UNITS - 1:
+                eight = blocksums.tile([P, 2, D], F32, name="eight")
+                nc.vector.tensor_tensor(out=eight[:], in0=sum4[block][:, 0:5:3, :],
+                                        in1=sum4[block][:, 1:5:3, :], op=ADD)
+                ten_bf[block] = blocksums.tile([P, 2, D], BF16, name="ten_bf", align_bytes=64)
+                nc.vector.tensor_tensor(out=ten_bf[block][:], in0=eight[:],
+                                        in1=sum2[BLOCK_UNITS * block + 2][:], op=ADD)
+
+        def round_sums(n):
+            block, place = divmod(n, BLOCK_UNITS)
+            nc.scalar.copy(out=to_quantise[n][:, 4:6, :], in_=sum2[n][:])
+            nc.scalar.copy(out=to_quantise[n][:, 6, :], in_=sum4[block][:, place, :])
+
+        def quantise_sums(n):
+            block, place = divmod(n, BLOCK_UNITS)
+            quantise(to_quantise[n][:, 4:6, :], codes[n][:, 4:6, :], scales[n][:, 4:6, :])
+            quantise(to_quantise[n][:, 6:7, :], codes[n][:, 6:7, :], scales[n][:, 6:7, :])
+            if place == BLOCK_UNITS - 1:
+                ten_codes[block] = blocksums.tile([P, 2, P], U32, name="ten_codes", align_bytes=64)
+                ten_scales[block] = blocksums.tile([P, 2, P], U8, name="ten_scales", align_bytes=64)
+                quantise(ten_bf[block][:], ten_codes[block][:], ten_scales[block][:])
+
+        def multiply(n):
+            block, place = divmod(n, BLOCK_UNITS)
+            biased[n] = pre.tile([P, OPERANDS, DO], F32, name="biased")
+            for first in range(0, OPERANDS, BANK_PASSES):
+                last = min(first + BANK_PASSES, OPERANDS)
+                acc = mps.tile([P, BANK_PASSES, DO], F32, name="acc")
+                for a in range(first, last):
+                    product(acc[:, a - first, :], codes[n][:, a, :], scales[n][:, a, :], OPERAND_SCALE[a])
+                nc.vector.tensor_tensor(out=biased[n][:, first:last, :], in0=acc[:, 0:last - first, :],
+                                        in1=unit_bias[:, first:last, :], op=ADD)
+            if place == BLOCK_UNITS - 1:
+                ten_biased[block] = pre.tile([P, 2, DO], F32, name="ten_biased")
+                acc = mps.tile([P, BANK_PASSES, DO], F32, name="acc")
+                for g in range(2):
+                    product(acc[:, g, :], ten_codes[block][:, g, :], ten_scales[block][:, g, :], 3)
+                nc.vector.tensor_tensor(out=ten_biased[block][:], in0=acc[:, 0:2, :], in1=ten_bias[:], op=ADD)
+
+        def finish(n):
+            block, place = divmod(n, BLOCK_UNITS)
+            pair, half = divmod(n, PAIR)
+            for scale in range(3):
+                groups = UNIT // GROUP[scale]
+                if half == 0:
+                    results[scale] = res.tile([P, PAIR * groups, COPIES[scale], DO], F32,
+                                              name="result%d" % scale)
+                first = FIRST_OPERAND[scale]
+                relu_and_repeat(scale, biased[n][:, first:first + groups, :],
+                                results[scale][:, half * groups:(half + 1) * groups, :, :])
+                if half == PAIR - 1:
+                    store(scale, PAIR * UNIT * pair, results[scale][:])
+            if place == BLOCK_UNITS - 1:
+                ten_result = res.tile([P, 2, COPIES[3], DO], F32, name="ten_result")
+                relu_and_repeat(3, ten_biased[block][:], ten_result[:])
+                store(3, BLOCK_UNITS * UNIT * block, ten_result[:])
+
+        load(0)
+
+        w_codes = const.tile([P, NS, DO], U32, name="w_codes", align_bytes=64)
+        nc.sync.dma_start(out=w_codes[:].bitcast(I32),
+                          in_=Ws_words.rearrange("s p o t -> p s (o t)").bitcast(I32))
+        w_scales = const.tile([P, NS, DO], U8, name="w_scales", align_bytes=64)
+        nc.vector.memset(w_scales[:].bitcast(I32), 0)
+        for quadrant in range(4):
+            nc.sync.dma_start(
+                out=w_scales[32 * quadrant:32 * quadrant + 4, :, :].bitcast(I32),
+                in_=Ws_scales[:, 4 * quadrant:4 * quadrant + 4, :].rearrange("s q o -> q s o").bitcast(I32),
+            )
+        for n in range(1, LOADS_AHEAD):
+            load(n)
+
+        ident = const.tile([P, P], F32, name="ident")
+        make_identity(nc, ident[:])
+
+        b_all = const.tile([P, NS * DO], BF16, name="b_all")
+        nc.scalar.dma_start(out=b_all[:], in_=bs.rearrange("s o -> (s o)").partition_broadcast(P))
+        unit_bias = const.tile([P, OPERANDS, DO], F32, name="unit_bias")
+        for a in range(OPERANDS):
+            s = OPERAND_SCALE[a]
+            nc.vector.tensor_copy(out=unit_bias[:, a, :], in_=b_all[:, DO * s:DO * (s + 1)])
+        ten_bias = const.tile([P, 2, DO], F32, name="ten_bias")
+        for g in range(2):
+            nc.vector.tensor_copy(out=ten_bias[:, g, :], in_=b_all[:, DO * 3:DO * 4])
+
+        for i in range(UNITS + 5):
+            if i + LOADS_AHEAD < UNITS:
+                load(i + LOADS_AHEAD)
+            if i < UNITS:
+                transpose(i)
+            if 0 <= i - 1 < UNITS:
+                quantise_x(i - 1)
+                add_rows(i - 1)
+            if 0 <= i - 2 < UNITS:
+                round_sums(i - 2)
+            if 0 <= i - 3 < UNITS:
+                quantise_sums(i - 3)
+            if 0 <= i - 4 < UNITS:
+                multiply(i - 4)
+            if 0 <= i - 5 < UNITS:
+                finish(i - 5)

@@ -42,7 +42,7 @@ def tile_contractexpand_pa_t_e_kernel(tc, inputs_c_e, Ws_words, Ws_scales, bs, o
     with tc.tile_pool(name="const", bufs=1) as const, \
             tc.tile_pool(name="xin", bufs=LOADS_AHEAD + 2) as xin, \
             tc.tile_pool(name="bf", bufs=5) as bf, \
-            tc.tile_pool(name="sums", bufs=5) as sums, \
+            tc.tile_pool(name="sums", bufs=6) as sums, \
             tc.tile_pool(name="blocksums", bufs=2) as blocksums, \
             tc.tile_pool(name="mx", bufs=5) as mx, \
             tc.tile_pool(name="pre", bufs=3) as pre, \
@@ -51,7 +51,7 @@ def tile_contractexpand_pa_t_e_kernel(tc, inputs_c_e, Ws_words, Ws_scales, bs, o
             tc.psum_pool(name="mps", bufs=4) as mps, \
             tc.manual_schedule():
 
-        x_nat, to_quantise, codes, scales = {}, {}, {}, {}
+        x_nat, transposed, to_quantise, codes, scales = {}, {}, {}, {}, {}
         sum2, sum4, ten_bf, ten_codes, ten_scales = {}, {}, {}, {}, {}
         biased, ten_biased, results = {}, {}, {}
 
@@ -98,6 +98,7 @@ def tile_contractexpand_pa_t_e_kernel(tc, inputs_c_e, Ws_words, Ws_scales, bs, o
             to_quantise[n] = bf.tile([P, OPERANDS, D], BF16, name="to_quantise", align_bytes=64)
             for half in range(UNIT // 2):
                 xt = tps.tile([P, 2, 2, P], F32, name="xt")
+                transposed[n, half] = xt
                 for t in range(2):
                     words = x_nat[n][:, 2 * half + t, :].bitcast(F32)
                     for u in range(2):
@@ -113,27 +114,36 @@ def tile_contractexpand_pa_t_e_kernel(tc, inputs_c_e, Ws_words, Ws_scales, bs, o
             scales[n] = mx.tile([P, OPERANDS, P], U8, name="scales", align_bytes=64)
             quantise(to_quantise[n][:, 0:4, :], codes[n][:, 0:4, :], scales[n][:, 0:4, :])
 
-        def add_rows(n):
-            block, place = divmod(n, BLOCK_UNITS)
+        def add_pairs(n):
             sum2[n] = sums.tile([P, 2, D], F32, name="sum2")
-            nc.vector.tensor_tensor(out=sum2[n][:], in0=to_quantise[n][:, 0:4:2, :],
-                                    in1=to_quantise[n][:, 1:4:2, :], op=ADD)
+            for half in range(UNIT // 2):
+                nc.vector.tensor_tensor(
+                    out=sum2[n][:, half, :].rearrange("p (r u e) -> p r u e", u=2, e=2),
+                    in0=transposed[n, half][:, 1, :, :].bitcast(BF16).rearrange("p u (r e) -> p r u e", e=2),
+                    in1=to_quantise[n][:, 2 * half, :].rearrange("p (r u e) -> p r u e", u=2, e=2),
+                    op=ADD,
+                )
+
+        def add_fours_and_tens(n):
+            block, place = divmod(n, BLOCK_UNITS)
             if place == 0:
                 sum4[block] = blocksums.tile([P, BLOCK_UNITS, D], F32, name="sum4")
-            nc.vector.tensor_tensor(out=sum4[block][:, place, :], in0=sum2[n][:, 0, :],
+            nc.gpsimd.tensor_tensor(out=sum4[block][:, place, :], in0=sum2[n][:, 0, :],
                                     in1=sum2[n][:, 1, :], op=ADD)
             if place == BLOCK_UNITS - 1:
                 eight = blocksums.tile([P, 2, D], F32, name="eight")
-                nc.vector.tensor_tensor(out=eight[:], in0=sum4[block][:, 0:5:3, :],
+                nc.gpsimd.tensor_tensor(out=eight[:], in0=sum4[block][:, 0:5:3, :],
                                         in1=sum4[block][:, 1:5:3, :], op=ADD)
                 ten_bf[block] = blocksums.tile([P, 2, D], BF16, name="ten_bf", align_bytes=64)
-                nc.vector.tensor_tensor(out=ten_bf[block][:], in0=eight[:],
+                nc.gpsimd.tensor_tensor(out=ten_bf[block][:], in0=eight[:],
                                         in1=sum2[BLOCK_UNITS * block + 2][:], op=ADD)
 
-        def round_sums(n):
-            block, place = divmod(n, BLOCK_UNITS)
+        def round_pairs(n):
             nc.scalar.copy(out=to_quantise[n][:, 4:6, :], in_=sum2[n][:])
-            nc.scalar.copy(out=to_quantise[n][:, 6, :], in_=sum4[block][:, place, :])
+
+        def round_four(n):
+            block, place = divmod(n, BLOCK_UNITS)
+            nc.vector.tensor_copy(out=to_quantise[n][:, 6, :], in_=sum4[block][:, place, :])
 
         def quantise_sums(n):
             block, place = divmod(n, BLOCK_UNITS)
@@ -212,11 +222,14 @@ def tile_contractexpand_pa_t_e_kernel(tc, inputs_c_e, Ws_words, Ws_scales, bs, o
                 load(i + LOADS_AHEAD)
             if i < UNITS:
                 transpose(i)
+            if 0 <= i - 3 < UNITS:
+                round_four(i - 3)
             if 0 <= i - 1 < UNITS:
                 quantise_x(i - 1)
-                add_rows(i - 1)
+                add_pairs(i - 1)
             if 0 <= i - 2 < UNITS:
-                round_sums(i - 2)
+                add_fours_and_tens(i - 2)
+                round_pairs(i - 2)
             if 0 <= i - 3 < UNITS:
                 quantise_sums(i - 3)
             if 0 <= i - 4 < UNITS:

@@ -20,7 +20,8 @@ SLOTS = N // P
 UNIT = 4
 UNITS = SLOTS // UNIT
 BLOCK_UNITS = 5
-BLOCKS = UNITS // BLOCK_UNITS
+TEN = GROUP[3]
+BLOCK_TENS = BLOCK_UNITS * UNIT // TEN
 PAIR = 2
 
 OPERAND_SCALE = (0, 0, 0, 0, 1, 1, 2)
@@ -43,8 +44,8 @@ def tile_contractexpand_pa_t_e_kernel(tc, inputs_c_e, Ws_words, Ws_scales, bs, o
             tc.tile_pool(name="xin", bufs=LOADS_AHEAD + 2) as xin, \
             tc.tile_pool(name="bf", bufs=5) as bf, \
             tc.tile_pool(name="sums", bufs=6) as sums, \
-            tc.tile_pool(name="blocksums", bufs=2) as blocksums, \
-            tc.tile_pool(name="mx", bufs=5) as mx, \
+            tc.tile_pool(name="tens", bufs=2) as tens, \
+            tc.tile_pool(name="mx", bufs=6) as mx, \
             tc.tile_pool(name="pre", bufs=3) as pre, \
             tc.tile_pool(name="res", bufs=3) as res, \
             tc.psum_pool(name="tps", bufs=4) as tps, \
@@ -53,7 +54,7 @@ def tile_contractexpand_pa_t_e_kernel(tc, inputs_c_e, Ws_words, Ws_scales, bs, o
 
         x_nat, transposed, to_quantise, codes, scales = {}, {}, {}, {}, {}
         sum2, sum4, ten_bf, ten_codes, ten_scales = {}, {}, {}, {}, {}
-        biased, ten_biased, results = {}, {}, {}
+        biased, ten_biased, results, running = {}, {}, {}, {}
 
         def load(n):
             x_nat[n] = xin.tile([P, UNIT, D], BF16, name="x_nat")
@@ -124,38 +125,40 @@ def tile_contractexpand_pa_t_e_kernel(tc, inputs_c_e, Ws_words, Ws_scales, bs, o
                     op=ADD,
                 )
 
+        def add_to_ten(first_slot, slots, piece):
+            block, place = divmod(first_slot // TEN, BLOCK_TENS)
+            if first_slot % TEN == 0:
+                running["ten"] = piece
+            elif (first_slot + slots) % TEN == 0:
+                if place == 0:
+                    ten_bf[block] = tens.tile([P, BLOCK_TENS, D], BF16, name="ten_bf", align_bytes=64)
+                nc.gpsimd.tensor_tensor(out=ten_bf[block][:, place, :], in0=running["ten"], in1=piece, op=ADD)
+            else:
+                partial = sums.tile([P, D], F32, name="partial")
+                nc.gpsimd.tensor_tensor(out=partial[:], in0=running["ten"], in1=piece, op=ADD)
+                running["ten"] = partial[:]
+
         def add_fours_and_tens(n):
-            block, place = divmod(n, BLOCK_UNITS)
-            if place == 0:
-                sum4[block] = blocksums.tile([P, BLOCK_UNITS, D], F32, name="sum4")
-            nc.gpsimd.tensor_tensor(out=sum4[block][:, place, :], in0=sum2[n][:, 0, :],
-                                    in1=sum2[n][:, 1, :], op=ADD)
-            if place == BLOCK_UNITS - 1:
-                eight = blocksums.tile([P, 2, D], F32, name="eight")
-                nc.gpsimd.tensor_tensor(out=eight[:], in0=sum4[block][:, 0:5:3, :],
-                                        in1=sum4[block][:, 1:5:3, :], op=ADD)
-                ten_bf[block] = blocksums.tile([P, 2, D], BF16, name="ten_bf", align_bytes=64)
-                nc.gpsimd.tensor_tensor(out=ten_bf[block][:], in0=eight[:],
-                                        in1=sum2[BLOCK_UNITS * block + 2][:], op=ADD)
+            sum4[n] = sums.tile([P, D], F32, name="sum4")
+            nc.gpsimd.tensor_tensor(out=sum4[n][:], in0=sum2[n][:, 0, :], in1=sum2[n][:, 1, :], op=ADD)
+            first_slot = UNIT * n
+            if first_slot // TEN == (first_slot + UNIT - 1) // TEN:
+                add_to_ten(first_slot, UNIT, sum4[n][:])
+            else:
+                add_to_ten(first_slot, 2, sum2[n][:, 0, :])
+                add_to_ten(first_slot + 2, 2, sum2[n][:, 1, :])
 
         def round_pairs(n):
             nc.scalar.copy(out=to_quantise[n][:, 4:6, :], in_=sum2[n][:])
 
         def round_four(n):
-            block, place = divmod(n, BLOCK_UNITS)
-            nc.vector.tensor_copy(out=to_quantise[n][:, 6, :], in_=sum4[block][:, place, :])
+            nc.vector.tensor_copy(out=to_quantise[n][:, 6, :], in_=sum4[n][:])
 
         def quantise_sums(n):
-            block, place = divmod(n, BLOCK_UNITS)
             quantise(to_quantise[n][:, 4:6, :], codes[n][:, 4:6, :], scales[n][:, 4:6, :])
             quantise(to_quantise[n][:, 6:7, :], codes[n][:, 6:7, :], scales[n][:, 6:7, :])
-            if place == BLOCK_UNITS - 1:
-                ten_codes[block] = blocksums.tile([P, 2, P], U32, name="ten_codes", align_bytes=64)
-                ten_scales[block] = blocksums.tile([P, 2, P], U8, name="ten_scales", align_bytes=64)
-                quantise(ten_bf[block][:], ten_codes[block][:], ten_scales[block][:])
 
         def multiply(n):
-            block, place = divmod(n, BLOCK_UNITS)
             biased[n] = pre.tile([P, OPERANDS, DO], F32, name="biased")
             for first in range(0, OPERANDS, BANK_PASSES):
                 last = min(first + BANK_PASSES, OPERANDS)
@@ -164,15 +167,8 @@ def tile_contractexpand_pa_t_e_kernel(tc, inputs_c_e, Ws_words, Ws_scales, bs, o
                     product(acc[:, a - first, :], codes[n][:, a, :], scales[n][:, a, :], OPERAND_SCALE[a])
                 nc.vector.tensor_tensor(out=biased[n][:, first:last, :], in0=acc[:, 0:last - first, :],
                                         in1=unit_bias[:, first:last, :], op=ADD)
-            if place == BLOCK_UNITS - 1:
-                ten_biased[block] = pre.tile([P, 2, DO], F32, name="ten_biased")
-                acc = mps.tile([P, BANK_PASSES, DO], F32, name="acc")
-                for g in range(2):
-                    product(acc[:, g, :], ten_codes[block][:, g, :], ten_scales[block][:, g, :], 3)
-                nc.vector.tensor_tensor(out=ten_biased[block][:], in0=acc[:, 0:2, :], in1=ten_bias[:], op=ADD)
 
         def finish(n):
-            block, place = divmod(n, BLOCK_UNITS)
             pair, half = divmod(n, PAIR)
             for scale in range(3):
                 groups = UNIT // GROUP[scale]
@@ -184,8 +180,28 @@ def tile_contractexpand_pa_t_e_kernel(tc, inputs_c_e, Ws_words, Ws_scales, bs, o
                                 results[scale][:, half * groups:(half + 1) * groups, :, :])
                 if half == PAIR - 1:
                     store(scale, PAIR * UNIT * pair, results[scale][:])
+
+        def quantise_tens(n):
+            block, place = divmod(n, BLOCK_UNITS)
             if place == BLOCK_UNITS - 1:
-                ten_result = res.tile([P, 2, COPIES[3], DO], F32, name="ten_result")
+                ten_codes[block] = tens.tile([P, BLOCK_TENS, P], U32, name="ten_codes", align_bytes=64)
+                ten_scales[block] = tens.tile([P, BLOCK_TENS, P], U8, name="ten_scales", align_bytes=64)
+                quantise(ten_bf[block][:], ten_codes[block][:], ten_scales[block][:])
+
+        def multiply_tens(n):
+            block, place = divmod(n, BLOCK_UNITS)
+            if place == BLOCK_UNITS - 1:
+                ten_biased[block] = pre.tile([P, BLOCK_TENS, DO], F32, name="ten_biased")
+                acc = mps.tile([P, BANK_PASSES, DO], F32, name="acc")
+                for g in range(BLOCK_TENS):
+                    product(acc[:, g, :], ten_codes[block][:, g, :], ten_scales[block][:, g, :], 3)
+                nc.vector.tensor_tensor(out=ten_biased[block][:], in0=acc[:, 0:BLOCK_TENS, :],
+                                        in1=ten_bias[:], op=ADD)
+
+        def finish_tens(n):
+            block, place = divmod(n, BLOCK_UNITS)
+            if place == BLOCK_UNITS - 1:
+                ten_result = res.tile([P, BLOCK_TENS, COPIES[3], DO], F32, name="ten_result")
                 relu_and_repeat(3, ten_biased[block][:], ten_result[:])
                 store(3, BLOCK_UNITS * UNIT * block, ten_result[:])
 
@@ -213,26 +229,25 @@ def tile_contractexpand_pa_t_e_kernel(tc, inputs_c_e, Ws_words, Ws_scales, bs, o
         for a in range(OPERANDS):
             s = OPERAND_SCALE[a]
             nc.vector.tensor_copy(out=unit_bias[:, a, :], in_=b_all[:, DO * s:DO * (s + 1)])
-        ten_bias = const.tile([P, 2, DO], F32, name="ten_bias")
-        for g in range(2):
+        ten_bias = const.tile([P, BLOCK_TENS, DO], F32, name="ten_bias")
+        for g in range(BLOCK_TENS):
             nc.vector.tensor_copy(out=ten_bias[:, g, :], in_=b_all[:, DO * 3:DO * 4])
 
-        for i in range(UNITS + 5):
-            if i + LOADS_AHEAD < UNITS:
-                load(i + LOADS_AHEAD)
-            if i < UNITS:
-                transpose(i)
-            if 0 <= i - 3 < UNITS:
-                round_four(i - 3)
-            if 0 <= i - 1 < UNITS:
-                quantise_x(i - 1)
-                add_pairs(i - 1)
-            if 0 <= i - 2 < UNITS:
-                add_fours_and_tens(i - 2)
-                round_pairs(i - 2)
-            if 0 <= i - 3 < UNITS:
-                quantise_sums(i - 3)
-            if 0 <= i - 4 < UNITS:
-                multiply(i - 4)
-            if 0 <= i - 5 < UNITS:
-                finish(i - 5)
+        def turn(stage, n):
+            if 0 <= n < UNITS:
+                stage(n)
+
+        for i in range(UNITS + 7):
+            turn(load, i + LOADS_AHEAD)
+            turn(transpose, i)
+            turn(add_pairs, i - 1)
+            turn(add_fours_and_tens, i - 1)
+            turn(multiply_tens, i - 3)
+            turn(multiply, i - 5)
+            turn(round_pairs, i - 2)
+            turn(round_four, i - 2)
+            turn(quantise_x, i - 1)
+            turn(quantise_tens, i - 2)
+            turn(quantise_sums, i - 3)
+            turn(finish_tens, i - 4)
+            turn(finish, i - 6)

@@ -22,7 +22,7 @@ UNITS = SLOTS // UNIT
 BLOCK_UNITS = 5
 TEN = GROUP[3]
 BLOCK_TENS = BLOCK_UNITS * UNIT // TEN
-PAIR = 2
+PAIR = 1
 
 OPERAND_SCALE = (0, 0, 0, 0, 1, 1, 2)
 OPERANDS = len(OPERAND_SCALE)
@@ -42,12 +42,13 @@ def tile_contractexpand_pa_t_e_kernel(tc, inputs_c_e, Ws_words, Ws_scales, bs, o
 
     with tc.tile_pool(name="const", bufs=1) as const, \
             tc.tile_pool(name="xin", bufs=LOADS_AHEAD + 2) as xin, \
-            tc.tile_pool(name="bf", bufs=5) as bf, \
+            tc.tile_pool(name="bf", bufs=6) as bf, \
             tc.tile_pool(name="sums", bufs=6) as sums, \
+            tc.tile_pool(name="fours", bufs=2) as fours, \
             tc.tile_pool(name="tens", bufs=2) as tens, \
-            tc.tile_pool(name="mx", bufs=6) as mx, \
+            tc.tile_pool(name="mx", bufs=7) as mx, \
             tc.tile_pool(name="pre", bufs=3) as pre, \
-            tc.tile_pool(name="res", bufs=3) as res, \
+            tc.tile_pool(name="res", bufs=6) as res, \
             tc.psum_pool(name="tps", bufs=4) as tps, \
             tc.psum_pool(name="mps", bufs=4) as mps, \
             tc.manual_schedule():
@@ -132,15 +133,17 @@ def tile_contractexpand_pa_t_e_kernel(tc, inputs_c_e, Ws_words, Ws_scales, bs, o
             elif (first_slot + slots) % TEN == 0:
                 if place == 0:
                     ten_bf[block] = tens.tile([P, BLOCK_TENS, D], BF16, name="ten_bf", align_bytes=64)
-                nc.gpsimd.tensor_tensor(out=ten_bf[block][:, place, :], in0=running["ten"], in1=piece, op=ADD)
+                nc.vector.tensor_tensor(out=ten_bf[block][:, place, :], in0=running["ten"], in1=piece, op=ADD)
             else:
                 partial = sums.tile([P, D], F32, name="partial")
-                nc.gpsimd.tensor_tensor(out=partial[:], in0=running["ten"], in1=piece, op=ADD)
+                nc.vector.tensor_tensor(out=partial[:], in0=running["ten"], in1=piece, op=ADD)
                 running["ten"] = partial[:]
 
-        def add_fours_and_tens(n):
-            sum4[n] = sums.tile([P, D], F32, name="sum4")
+        def add_four(n):
+            sum4[n] = fours.tile([P, D], F32, name="sum4")
             nc.gpsimd.tensor_tensor(out=sum4[n][:], in0=sum2[n][:, 0, :], in1=sum2[n][:, 1, :], op=ADD)
+
+        def add_tens(n):
             first_slot = UNIT * n
             if first_slot // TEN == (first_slot + UNIT - 1) // TEN:
                 add_to_ten(first_slot, UNIT, sum4[n][:])
@@ -237,17 +240,18 @@ def tile_contractexpand_pa_t_e_kernel(tc, inputs_c_e, Ws_words, Ws_scales, bs, o
             if 0 <= n < UNITS:
                 stage(n)
 
-        for i in range(UNITS + 7):
+        for i in range(UNITS + 8):
             turn(load, i + LOADS_AHEAD)
             turn(transpose, i)
             turn(add_pairs, i - 1)
-            turn(add_fours_and_tens, i - 1)
-            turn(multiply_tens, i - 3)
-            turn(multiply, i - 5)
+            turn(multiply_tens, i - 5)
+            turn(multiply, i - 6)
             turn(round_pairs, i - 2)
-            turn(round_four, i - 2)
+            turn(add_tens, i - 2)
             turn(quantise_x, i - 1)
-            turn(quantise_tens, i - 2)
-            turn(quantise_sums, i - 3)
-            turn(finish_tens, i - 4)
-            turn(finish, i - 6)
+            turn(quantise_tens, i - 3)
+            turn(quantise_sums, i - 4)
+            turn(round_four, i - 3)
+            turn(add_four, i - 1)
+            turn(finish_tens, i - 6)
+            turn(finish, i - 7)

@@ -59,7 +59,10 @@ def tile_contractexpand_pa_t_e_kernel(tc, inputs_c_e, Ws_words, Ws_scales, bs, o
 
         def load(n):
             x_nat[n] = xin.tile([P, UNIT, D], BF16, name="x_nat")
-            nc.sync.dma_start(out=x_nat[n][:], in_=x_slots[:, UNIT * n:UNIT * (n + 1), :])
+            step = UNIT // 2 if n == 0 else UNIT
+            for t in range(0, UNIT, step):
+                nc.sync.dma_start(out=x_nat[n][:, t:t + step, :],
+                                  in_=x_slots[:, UNIT * n + t:UNIT * n + t + step, :])
 
         def quantise(values, words, plane):
             nc.vector.quantize_mx(
@@ -208,7 +211,11 @@ def tile_contractexpand_pa_t_e_kernel(tc, inputs_c_e, Ws_words, Ws_scales, bs, o
                 relu_and_repeat(3, ten_biased[block][:], ten_result[:])
                 store(3, BLOCK_UNITS * UNIT * block, ten_result[:])
 
-        load(0)
+        for n in range(LOADS_AHEAD):
+            load(n)
+
+        ident = const.tile([P, P], F32, name="ident")
+        make_identity(nc, ident[:])
 
         w_codes = const.tile([P, NS, DO], U32, name="w_codes", align_bytes=64)
         nc.sync.dma_start(out=w_codes[:].bitcast(I32),
@@ -220,21 +227,19 @@ def tile_contractexpand_pa_t_e_kernel(tc, inputs_c_e, Ws_words, Ws_scales, bs, o
                 out=w_scales[32 * quadrant:32 * quadrant + 4, :, :].bitcast(I32),
                 in_=Ws_scales[:, 4 * quadrant:4 * quadrant + 4, :].rearrange("s q o -> q s o").bitcast(I32),
             )
-        for n in range(1, LOADS_AHEAD):
-            load(n)
-
-        ident = const.tile([P, P], F32, name="ident")
-        make_identity(nc, ident[:])
 
         b_all = const.tile([P, NS * DO], BF16, name="b_all")
-        nc.scalar.dma_start(out=b_all[:], in_=bs.rearrange("s o -> (s o)").partition_broadcast(P))
+        nc.sync.dma_start(out=b_all[:], in_=bs.rearrange("s o -> (s o)").partition_broadcast(P))
         unit_bias = const.tile([P, OPERANDS, DO], F32, name="unit_bias")
-        for a in range(OPERANDS):
-            s = OPERAND_SCALE[a]
-            nc.vector.tensor_copy(out=unit_bias[:, a, :], in_=b_all[:, DO * s:DO * (s + 1)])
         ten_bias = const.tile([P, BLOCK_TENS, DO], F32, name="ten_bias")
-        for g in range(BLOCK_TENS):
-            nc.vector.tensor_copy(out=ten_bias[:, g, :], in_=b_all[:, DO * 3:DO * 4])
+
+        def convert_bias(n):
+            if n == 0:
+                for a in range(OPERANDS):
+                    s = OPERAND_SCALE[a]
+                    nc.vector.tensor_copy(out=unit_bias[:, a, :], in_=b_all[:, DO * s:DO * (s + 1)])
+                for g in range(BLOCK_TENS):
+                    nc.vector.tensor_copy(out=ten_bias[:, g, :], in_=b_all[:, DO * 3:DO * 4])
 
         def turn(stage, n):
             if 0 <= n < UNITS:
@@ -244,6 +249,7 @@ def tile_contractexpand_pa_t_e_kernel(tc, inputs_c_e, Ws_words, Ws_scales, bs, o
             turn(load, i + LOADS_AHEAD)
             turn(transpose, i)
             turn(add_pairs, i - 1)
+            turn(convert_bias, i - 5)
             turn(multiply_tens, i - 5)
             turn(multiply, i - 6)
             turn(round_pairs, i - 2)

@@ -8,6 +8,7 @@ U32 = mybir.dt.uint32
 U8 = mybir.dt.uint8
 FP8X4 = mybir.dt.float8_e4m3fn_x4
 ADD = mybir.AluOpType.add
+MULT = mybir.AluOpType.mult
 RELU = mybir.ActivationFunctionType.Relu
 
 P = 128
@@ -21,16 +22,8 @@ UNIT = 4
 UNITS = SLOTS // UNIT
 BLOCK_UNITS = 5
 TEN = GROUP[3]
-BLOCK_TENS = BLOCK_UNITS * UNIT // TEN
-PAIR = 1
-
-OPERAND_SCALE = (0, 0, 0, 0, 1, 1, 2)
-OPERANDS = len(OPERAND_SCALE)
-FIRST_OPERAND = (0, 4, 6)
-BANK_PASSES = 4
-
-COPIES = (1, 2, 2, 2)
-
+PLACES = 8
+COPIES = 2
 LOADS_AHEAD = 8
 FLOPS = 2 * D * DO * sum(N // r for r in GROUP)
 
@@ -43,19 +36,21 @@ def tile_contractexpand_pa_t_e_kernel(tc, inputs_c_e, Ws_words, Ws_scales, bs, o
     with tc.tile_pool(name="const", bufs=1) as const, \
             tc.tile_pool(name="xin", bufs=LOADS_AHEAD + 2) as xin, \
             tc.tile_pool(name="bf", bufs=6) as bf, \
-            tc.tile_pool(name="sums", bufs=6) as sums, \
+            tc.tile_pool(name="sums", bufs=3) as sums, \
             tc.tile_pool(name="fours", bufs=2) as fours, \
-            tc.tile_pool(name="tens", bufs=2) as tens, \
             tc.tile_pool(name="mx", bufs=7) as mx, \
-            tc.tile_pool(name="pre", bufs=3) as pre, \
-            tc.tile_pool(name="res", bufs=6) as res, \
+            tc.tile_pool(name="acts", bufs=2) as acts, \
+            tc.tile_pool(name="res", bufs=4) as res, \
             tc.psum_pool(name="tps", bufs=4) as tps, \
-            tc.psum_pool(name="mps", bufs=4) as mps, \
+            tc.psum_pool(name="mps", bufs=2) as mps, \
+            tc.psum_pool(name="bps", bufs=2) as bps, \
             tc.manual_schedule():
 
         x_nat, transposed, to_quantise, codes, scales = {}, {}, {}, {}, {}
-        sum2, sum4, ten_bf, ten_codes, ten_scales = {}, {}, {}, {}, {}
-        biased, ten_biased, results, running = {}, {}, {}, {}
+        sum2, sum4, running, hidden = {}, {}, {}, {}
+
+        def has_ten(n):
+            return n % BLOCK_UNITS in (2, 4)
 
         def load(n):
             x_nat[n] = xin.tile([P, UNIT, D], BF16, name="x_nat")
@@ -64,79 +59,59 @@ def tile_contractexpand_pa_t_e_kernel(tc, inputs_c_e, Ws_words, Ws_scales, bs, o
                 nc.sync.dma_start(out=x_nat[n][:, t:t + step, :],
                                   in_=x_slots[:, UNIT * n + t:UNIT * n + t + step, :])
 
-        def quantise(values, words, plane):
+        def quantise(n, first, last):
             nc.vector.quantize_mx(
-                out=words.rearrange("p a c -> p (a c)").bitcast(FP8X4),
-                scales=plane.rearrange("p a c -> p (a c)"),
-                in_=values.rearrange("p a c -> p (a c)"),
+                out=codes[n][:, first:last, :].rearrange("p a c -> p (a c)").bitcast(FP8X4),
+                scales=scales[n][:, first:last, :].rearrange("p a c -> p (a c)"),
+                in_=to_quantise[n][:, first:last, :].rearrange("p a c -> p (a c)"),
             )
 
-        def product(acc, words, plane, scale):
+        def product(acc, n, first, last, scale):
             nc.tensor.matmul_mx(
                 out=acc,
-                lhsT=words.bitcast(FP8X4),
-                lhsT_scale=plane,
-                rhs=w_codes[:, scale, :].bitcast(FP8X4),
-                rhs_scale=w_scales[:, scale, :],
+                lhsT=w_codes[:, scale, :].bitcast(FP8X4),
+                lhsT_scale=w_scales[:, scale, :],
+                rhs=codes[n][:, first:last, :].rearrange("p a c -> p (a c)").bitcast(FP8X4),
+                rhs_scale=scales[n][:, first:last, :].rearrange("p a c -> p (a c)"),
                 start=True,
                 stop=True,
             )
 
-        def relu_and_repeat(scale, values, target):
-            groups = values.shape[1]
-            nc.scalar.activation(
-                out=target,
-                in_=values.unsqueeze(2).to_broadcast([P, groups, COPIES[scale], DO]),
-                func=RELU,
-                scale=1.0 / GROUP[scale],
-            )
-
-        def store(scale, first_slot, tile_):
-            r, c = GROUP[scale], COPIES[scale]
-            slots = tile_.shape[1] * r
-            rows = out_slots[scale][:, first_slot:first_slot + slots, :].rearrange(
-                "p (g k c) d -> p g k (c d)", k=r // c, c=c)
-            for k in range(r // c):
-                nc.sync.dma_start(out=rows[:, :, k, :], in_=tile_.rearrange("p g c d -> p g (c d)"))
+        def bias_relu(target, acc, scale):
+            nc.scalar.activation(out=target, in_=acc, func=RELU, bias=bias_r[:, scale:scale + 1],
+                                 scale=1.0 / GROUP[scale])
 
         def transpose(n):
-            to_quantise[n] = bf.tile([P, OPERANDS, D], BF16, name="to_quantise", align_bytes=64)
-            for half in range(UNIT // 2):
+            to_quantise[n] = bf.tile([P, PLACES, D], BF16, name="to_quantise", align_bytes=64)
+            for odd in range(2):
                 xt = tps.tile([P, 2, 2, P], F32, name="xt")
-                transposed[n, half] = xt
-                for t in range(2):
-                    words = x_nat[n][:, 2 * half + t, :].bitcast(F32)
+                transposed[n, odd] = xt
+                for pair in range(2):
+                    words = x_nat[n][:, 2 * pair + odd, :].bitcast(F32)
                     for u in range(2):
-                        nc.tensor.transpose(xt[:, t, u, :], words[:, u:D // 2:2], ident[:])
+                        nc.tensor.transpose(xt[:, u, pair, :], words[:, u:D // 2:2], ident[:])
                 nc.scalar.copy(
-                    out=to_quantise[n][:, 2 * half:2 * half + 2, :].bitcast(F32).rearrange(
-                        "p t (r u) -> p t r u", u=2),
-                    in_=xt[:].rearrange("p t u r -> p t r u"),
+                    out=to_quantise[n][:, 2 * odd:2 * odd + 2, :].rearrange("p a c -> p (a c)").bitcast(
+                        F32).rearrange("p (x u) -> p x u", u=2),
+                    in_=xt[:].rearrange("p u a r -> p (a r) u"),
                 )
-
-        def quantise_x(n):
-            codes[n] = mx.tile([P, OPERANDS, P], U32, name="codes", align_bytes=64)
-            scales[n] = mx.tile([P, OPERANDS, P], U8, name="scales", align_bytes=64)
-            quantise(to_quantise[n][:, 0:4, :], codes[n][:, 0:4, :], scales[n][:, 0:4, :])
 
         def add_pairs(n):
             sum2[n] = sums.tile([P, 2, D], F32, name="sum2")
-            for half in range(UNIT // 2):
-                nc.vector.tensor_tensor(
-                    out=sum2[n][:, half, :].rearrange("p (r u e) -> p r u e", u=2, e=2),
-                    in0=transposed[n, half][:, 1, :, :].bitcast(BF16).rearrange("p u (r e) -> p r u e", e=2),
-                    in1=to_quantise[n][:, 2 * half, :].rearrange("p (r u e) -> p r u e", u=2, e=2),
-                    op=ADD,
-                )
+            odd = transposed[n, 1][:].rearrange("p u a r -> p u (a r)").bitcast(BF16).rearrange(
+                "p u (x e) -> p x u e", e=2)
+            even = to_quantise[n][:, 0:2, :].rearrange("p a (r u e) -> p (a r) u e", u=2, e=2)
+            nc.vector.tensor_tensor(out=sum2[n][:].rearrange("p a (r u e) -> p (a r) u e", u=2, e=2),
+                                    in0=odd, in1=even, op=ADD)
+            nc.vector.tensor_tensor(
+                out=to_quantise[n][:, 4:6, :].rearrange("p a (r u e) -> p (a r) u e", u=2, e=2),
+                in0=odd, in1=even, op=ADD)
 
-        def add_to_ten(first_slot, slots, piece):
-            block, place = divmod(first_slot // TEN, BLOCK_TENS)
+        def add_to_ten(n, first_slot, slots, piece):
             if first_slot % TEN == 0:
                 running["ten"] = piece
             elif (first_slot + slots) % TEN == 0:
-                if place == 0:
-                    ten_bf[block] = tens.tile([P, BLOCK_TENS, D], BF16, name="ten_bf", align_bytes=64)
-                nc.vector.tensor_tensor(out=ten_bf[block][:, place, :], in0=running["ten"], in1=piece, op=ADD)
+                nc.vector.tensor_tensor(out=to_quantise[n][:, 7, :], in0=running["ten"], in1=piece, op=ADD)
             else:
                 partial = sums.tile([P, D], F32, name="partial")
                 nc.vector.tensor_tensor(out=partial[:], in0=running["ten"], in1=piece, op=ADD)
@@ -149,67 +124,67 @@ def tile_contractexpand_pa_t_e_kernel(tc, inputs_c_e, Ws_words, Ws_scales, bs, o
         def add_tens(n):
             first_slot = UNIT * n
             if first_slot // TEN == (first_slot + UNIT - 1) // TEN:
-                add_to_ten(first_slot, UNIT, sum4[n][:])
+                add_to_ten(n, first_slot, UNIT, sum4[n][:])
             else:
-                add_to_ten(first_slot, 2, sum2[n][:, 0, :])
-                add_to_ten(first_slot + 2, 2, sum2[n][:, 1, :])
-
-        def round_pairs(n):
-            nc.scalar.copy(out=to_quantise[n][:, 4:6, :], in_=sum2[n][:])
+                add_to_ten(n, first_slot, 2, sum2[n][:, 0, :])
+                add_to_ten(n, first_slot + 2, 2, sum2[n][:, 1, :])
 
         def round_four(n):
             nc.vector.tensor_copy(out=to_quantise[n][:, 6, :], in_=sum4[n][:])
 
+        def quantise_x(n):
+            codes[n] = mx.tile([P, PLACES, P], U32, name="codes", align_bytes=64)
+            scales[n] = mx.tile([P, PLACES, P], U8, name="scales", align_bytes=64)
+            quantise(n, 0, 4)
+
         def quantise_sums(n):
-            quantise(to_quantise[n][:, 4:6, :], codes[n][:, 4:6, :], scales[n][:, 4:6, :])
-            quantise(to_quantise[n][:, 6:7, :], codes[n][:, 6:7, :], scales[n][:, 6:7, :])
+            if has_ten(n):
+                quantise(n, 4, 8)
+            else:
+                quantise(n, 4, 6)
+                quantise(n, 6, 7)
 
         def multiply(n):
-            biased[n] = pre.tile([P, OPERANDS, DO], F32, name="biased")
-            for first in range(0, OPERANDS, BANK_PASSES):
-                last = min(first + BANK_PASSES, OPERANDS)
-                acc = mps.tile([P, BANK_PASSES, DO], F32, name="acc")
-                for a in range(first, last):
-                    product(acc[:, a - first, :], codes[n][:, a, :], scales[n][:, a, :], OPERAND_SCALE[a])
-                nc.vector.tensor_tensor(out=biased[n][:, first:last, :], in0=acc[:, 0:last - first, :],
-                                        in1=unit_bias[:, first:last, :], op=ADD)
+            acc = mps.tile([P, UNIT * P], F32, name="acc")
+            product(acc[:], n, 0, 4, 0)
+            hidden[n, 0] = acts.tile([P, UNIT * P], F32, name="hidden_x")
+            bias_relu(hidden[n, 0][:], acc[:], 0)
+            acc = mps.tile([P, UNIT * P], F32, name="acc")
+            hidden[n, 1] = acts.tile([P, UNIT * P], F32, name="hidden_sums")
+            product(acc[:, 0:2 * P], n, 4, 6, 1)
+            product(acc[:, 2 * P:3 * P], n, 6, 7, 2)
+            if has_ten(n):
+                product(acc[:, 3 * P:4 * P], n, 7, 8, 3)
+            bias_relu(hidden[n, 1][:, 0:2 * P], acc[:, 0:2 * P], 1)
+            bias_relu(hidden[n, 1][:, 2 * P:3 * P], acc[:, 2 * P:3 * P], 2)
+            if has_ten(n):
+                bias_relu(hidden[n, 1][:, 3 * P:4 * P], acc[:, 3 * P:4 * P], 3)
 
-        def finish(n):
-            pair, half = divmod(n, PAIR)
-            for scale in range(3):
-                groups = UNIT // GROUP[scale]
-                if half == 0:
-                    results[scale] = res.tile([P, PAIR * groups, COPIES[scale], DO], F32,
-                                              name="result%d" % scale)
-                first = FIRST_OPERAND[scale]
-                relu_and_repeat(scale, biased[n][:, first:first + groups, :],
-                                results[scale][:, half * groups:(half + 1) * groups, :, :])
-                if half == PAIR - 1:
-                    store(scale, PAIR * UNIT * pair, results[scale][:])
+        def repeat_store(scale, first_slot, copies):
+            r = GROUP[scale]
+            rows = out_slots[scale][:, first_slot:first_slot + r, :].rearrange("p (k c) d -> p k (c d)", c=COPIES)
+            nc.sync.dma_start(out=rows, in_=copies.unsqueeze(1).to_broadcast([P, r // COPIES, COPIES * DO]))
 
-        def quantise_tens(n):
-            block, place = divmod(n, BLOCK_UNITS)
-            if place == BLOCK_UNITS - 1:
-                ten_codes[block] = tens.tile([P, BLOCK_TENS, P], U32, name="ten_codes", align_bytes=64)
-                ten_scales[block] = tens.tile([P, BLOCK_TENS, P], U8, name="ten_scales", align_bytes=64)
-                quantise(ten_bf[block][:], ten_codes[block][:], ten_scales[block][:])
+        def back(n):
+            turned = bps.tile([P, UNIT, DO], F32, name="turned")
+            for a in range(UNIT):
+                nc.tensor.transpose(turned[:, 2 * (a % 2) + a // 2, :], hidden[n, 0][:, a * P:(a + 1) * P], ident[:])
+            result_x = res.tile([P, UNIT, DO], F32, name="result_x")
+            nc.scalar.copy(out=result_x[:], in_=turned[:])
+            nc.sync.dma_start(out=out_slots[0][:, UNIT * n:UNIT * (n + 1), :], in_=result_x[:])
 
-        def multiply_tens(n):
-            block, place = divmod(n, BLOCK_UNITS)
-            if place == BLOCK_UNITS - 1:
-                ten_biased[block] = pre.tile([P, BLOCK_TENS, DO], F32, name="ten_biased")
-                acc = mps.tile([P, BANK_PASSES, DO], F32, name="acc")
-                for g in range(BLOCK_TENS):
-                    product(acc[:, g, :], ten_codes[block][:, g, :], ten_scales[block][:, g, :], 3)
-                nc.vector.tensor_tensor(out=ten_biased[block][:], in0=acc[:, 0:BLOCK_TENS, :],
-                                        in1=ten_bias[:], op=ADD)
-
-        def finish_tens(n):
-            block, place = divmod(n, BLOCK_UNITS)
-            if place == BLOCK_UNITS - 1:
-                ten_result = res.tile([P, BLOCK_TENS, COPIES[3], DO], F32, name="ten_result")
-                relu_and_repeat(3, ten_biased[block][:], ten_result[:])
-                store(3, BLOCK_UNITS * UNIT * block, ten_result[:])
+            places = 4 if has_ten(n) else 3
+            turned = bps.tile([P, UNIT, DO], F32, name="turned")
+            for a in range(places):
+                nc.tensor.transpose(turned[:, a, :], hidden[n, 1][:, a * P:(a + 1) * P], ident[:])
+            result_sums = res.tile([P, UNIT, COPIES, DO], F32, name="result_sums")
+            nc.scalar.copy(out=result_sums[:, 0:places, :, :],
+                           in_=turned[:, 0:places, :].unsqueeze(2).to_broadcast([P, places, COPIES, DO]))
+            nc.sync.dma_start(out=out_slots[1][:, UNIT * n:UNIT * (n + 1), :],
+                              in_=result_sums[:, 0:2, :, :].rearrange("p g c d -> p (g c) d"))
+            repeat_store(2, UNIT * n, result_sums[:, 2, :, :].rearrange("p c d -> p (c d)"))
+            if has_ten(n):
+                repeat_store(3, TEN * ((UNIT * n) // TEN), result_sums[:, 3, :, :].rearrange("p c d -> p (c d)"))
 
         for n in range(LOADS_AHEAD):
             load(n)
@@ -228,18 +203,20 @@ def tile_contractexpand_pa_t_e_kernel(tc, inputs_c_e, Ws_words, Ws_scales, bs, o
                 in_=Ws_scales[:, 4 * quadrant:4 * quadrant + 4, :].rearrange("s q o -> q s o").bitcast(I32),
             )
 
-        b_all = const.tile([P, NS * DO], BF16, name="b_all")
-        nc.sync.dma_start(out=b_all[:], in_=bs.rearrange("s o -> (s o)").partition_broadcast(P))
-        unit_bias = const.tile([P, OPERANDS, DO], F32, name="unit_bias")
-        ten_bias = const.tile([P, BLOCK_TENS, DO], F32, name="ten_bias")
+        b_rows = const.tile([P, P], BF16, name="b_rows")
+        nc.vector.memset(b_rows[:], 0.0)
+        nc.sync.dma_start(out=b_rows[0:NS, :], in_=bs)
+        b_wide = const.tile([P, P], F32, name="b_wide")
+        bias_r = const.tile([P, NS], F32, name="bias_r")
 
-        def convert_bias(n):
+        def prepare_bias(n):
             if n == 0:
-                for a in range(OPERANDS):
-                    s = OPERAND_SCALE[a]
-                    nc.vector.tensor_copy(out=unit_bias[:, a, :], in_=b_all[:, DO * s:DO * (s + 1)])
-                for g in range(BLOCK_TENS):
-                    nc.vector.tensor_copy(out=ten_bias[:, g, :], in_=b_all[:, DO * 3:DO * 4])
+                nc.vector.tensor_copy(out=b_wide[:], in_=b_rows[:])
+                b_turned = bps.tile([P, UNIT, DO], F32, name="turned")
+                nc.tensor.transpose(b_turned[:, 0, :], b_wide[:], ident[:])
+                for s in range(NS):
+                    nc.vector.tensor_scalar(out=bias_r[:, s:s + 1], in0=b_turned[:, 0, s:s + 1],
+                                            scalar1=1.0 / GROUP[s], scalar2=None, op0=MULT)
 
         def turn(stage, n):
             if 0 <= n < UNITS:
@@ -248,16 +225,12 @@ def tile_contractexpand_pa_t_e_kernel(tc, inputs_c_e, Ws_words, Ws_scales, bs, o
         for i in range(UNITS + 8):
             turn(load, i + LOADS_AHEAD)
             turn(transpose, i)
-            turn(add_pairs, i - 1)
-            turn(convert_bias, i - 5)
-            turn(multiply_tens, i - 5)
+            turn(prepare_bias, i - 5)
+            turn(back, i - 7)
             turn(multiply, i - 6)
-            turn(round_pairs, i - 2)
+            turn(add_pairs, i - 1)
             turn(add_tens, i - 2)
             turn(quantise_x, i - 1)
-            turn(quantise_tens, i - 3)
             turn(quantise_sums, i - 4)
             turn(round_four, i - 3)
             turn(add_four, i - 1)
-            turn(finish_tens, i - 6)
-            turn(finish, i - 7)

@@ -25,6 +25,7 @@ TEN = GROUP[3]
 PLACES = 8
 COPIES = 2
 LOADS_AHEAD = 8
+LOADS_FIRST = 3
 FLOPS = 2 * D * DO * sum(N // r for r in GROUP)
 
 
@@ -144,11 +145,13 @@ def tile_contractexpand_pa_t_e_kernel(tc, inputs_c_e, Ws_words, Ws_scales, bs, o
                 quantise(n, 4, 6)
                 quantise(n, 6, 7)
 
-        def multiply(n):
+        def multiply_x(n):
             acc = mps.tile([P, UNIT * P], F32, name="acc")
             product(acc[:], n, 0, 4, 0)
             hidden[n, 0] = acts.tile([P, UNIT * P], F32, name="hidden_x")
             bias_relu(hidden[n, 0][:], acc[:], 0)
+
+        def multiply_sums(n):
             acc = mps.tile([P, UNIT * P], F32, name="acc")
             hidden[n, 1] = acts.tile([P, UNIT * P], F32, name="hidden_sums")
             product(acc[:, 0:2 * P], n, 4, 6, 1)
@@ -165,7 +168,7 @@ def tile_contractexpand_pa_t_e_kernel(tc, inputs_c_e, Ws_words, Ws_scales, bs, o
             rows = out_slots[scale][:, first_slot:first_slot + r, :].rearrange("p (k c) d -> p k (c d)", c=COPIES)
             nc.sync.dma_start(out=rows, in_=copies.unsqueeze(1).to_broadcast([P, r // COPIES, COPIES * DO]))
 
-        def back(n):
+        def back_x(n):
             turned = bps.tile([P, UNIT, DO], F32, name="turned")
             for a in range(UNIT):
                 nc.tensor.transpose(turned[:, 2 * (a % 2) + a // 2, :], hidden[n, 0][:, a * P:(a + 1) * P], ident[:])
@@ -173,6 +176,7 @@ def tile_contractexpand_pa_t_e_kernel(tc, inputs_c_e, Ws_words, Ws_scales, bs, o
             nc.scalar.copy(out=result_x[:], in_=turned[:])
             nc.sync.dma_start(out=out_slots[0][:, UNIT * n:UNIT * (n + 1), :], in_=result_x[:])
 
+        def back_sums(n):
             places = 4 if has_ten(n) else 3
             turned = bps.tile([P, UNIT, DO], F32, name="turned")
             for a in range(places):
@@ -186,7 +190,7 @@ def tile_contractexpand_pa_t_e_kernel(tc, inputs_c_e, Ws_words, Ws_scales, bs, o
             if has_ten(n):
                 repeat_store(3, TEN * ((UNIT * n) // TEN), result_sums[:, 3, :, :].rearrange("p c d -> p (c d)"))
 
-        for n in range(LOADS_AHEAD):
+        for n in range(LOADS_FIRST):
             load(n)
 
         ident = const.tile([P, P], F32, name="ident")
@@ -206,6 +210,8 @@ def tile_contractexpand_pa_t_e_kernel(tc, inputs_c_e, Ws_words, Ws_scales, bs, o
         b_rows = const.tile([P, P], BF16, name="b_rows")
         nc.vector.memset(b_rows[:], 0.0)
         nc.sync.dma_start(out=b_rows[0:NS, :], in_=bs)
+        for n in range(LOADS_FIRST, LOADS_AHEAD):
+            load(n)
         b_wide = const.tile([P, P], F32, name="b_wide")
         bias_r = const.tile([P, NS], F32, name="bias_r")
 
@@ -225,9 +231,11 @@ def tile_contractexpand_pa_t_e_kernel(tc, inputs_c_e, Ws_words, Ws_scales, bs, o
         for i in range(UNITS + 8):
             turn(load, i + LOADS_AHEAD)
             turn(transpose, i)
-            turn(prepare_bias, i - 5)
-            turn(back, i - 7)
-            turn(multiply, i - 6)
+            turn(prepare_bias, i - 2)
+            turn(back_x, i - 4)
+            turn(back_sums, i - 6)
+            turn(multiply_x, i - 3)
+            turn(multiply_sums, i - 5)
             turn(add_pairs, i - 1)
             turn(add_tens, i - 2)
             turn(quantise_x, i - 1)

@@ -25,6 +25,7 @@ TEN = GROUP[3]
 PLACES = 8
 COPIES = 2
 LOADS_AHEAD = 8
+SCALAR_ROUNDS = 2
 LOADS_FIRST = 3
 FLOPS = 2 * D * DO * sum(N // r for r in GROUP)
 
@@ -42,9 +43,10 @@ def tile_contractexpand_pa_t_e_kernel(tc, inputs_c_e, Ws_words, Ws_scales, bs, o
             tc.tile_pool(name="mx", bufs=7) as mx, \
             tc.tile_pool(name="acts", bufs=2) as acts, \
             tc.tile_pool(name="res", bufs=4) as res, \
-            tc.psum_pool(name="tps", bufs=4) as tps, \
-            tc.psum_pool(name="mps", bufs=2) as mps, \
-            tc.psum_pool(name="bps", bufs=2) as bps, \
+            tc.psum_pool(name="even_ps", bufs=1) as even_ps, \
+            tc.psum_pool(name="odd_ps", bufs=3) as odd_ps, \
+            tc.psum_pool(name="acc_ps", bufs=1) as acc_ps, \
+            tc.psum_pool(name="turned_ps", bufs=1) as turned_ps, \
             tc.manual_schedule():
 
         x_nat, transposed, to_quantise, codes, scales = {}, {}, {}, {}, {}
@@ -55,10 +57,11 @@ def tile_contractexpand_pa_t_e_kernel(tc, inputs_c_e, Ws_words, Ws_scales, bs, o
 
         def load(n):
             x_nat[n] = xin.tile([P, UNIT, D], BF16, name="x_nat")
-            step = UNIT // 2 if n == 0 else UNIT
-            for t in range(0, UNIT, step):
-                nc.sync.dma_start(out=x_nat[n][:, t:t + step, :],
-                                  in_=x_slots[:, UNIT * n + t:UNIT * n + t + step, :])
+            if n == 0:
+                for t in (0, 2, 1, 3):
+                    nc.sync.dma_start(out=x_nat[n][:, t, :], in_=x_slots[:, t, :])
+            else:
+                nc.sync.dma_start(out=x_nat[n][:], in_=x_slots[:, UNIT * n:UNIT * (n + 1), :])
 
         def quantise(n, first, last):
             nc.vector.quantize_mx(
@@ -85,7 +88,7 @@ def tile_contractexpand_pa_t_e_kernel(tc, inputs_c_e, Ws_words, Ws_scales, bs, o
         def transpose(n):
             to_quantise[n] = bf.tile([P, PLACES, D], BF16, name="to_quantise", align_bytes=64)
             for odd in range(2):
-                xt = tps.tile([P, 2, 2, P], F32, name="xt")
+                xt = (odd_ps if odd else even_ps).tile([P, 2, 2, P], F32, name="xt")
                 transposed[n, odd] = xt
                 for pair in range(2):
                     words = x_nat[n][:, 2 * pair + odd, :].bitcast(F32)
@@ -104,9 +107,12 @@ def tile_contractexpand_pa_t_e_kernel(tc, inputs_c_e, Ws_words, Ws_scales, bs, o
             even = to_quantise[n][:, 0:2, :].rearrange("p a (r u e) -> p (a r) u e", u=2, e=2)
             nc.vector.tensor_tensor(out=sum2[n][:].rearrange("p a (r u e) -> p (a r) u e", u=2, e=2),
                                     in0=odd, in1=even, op=ADD)
-            nc.vector.tensor_tensor(
-                out=to_quantise[n][:, 4:6, :].rearrange("p a (r u e) -> p (a r) u e", u=2, e=2),
-                in0=odd, in1=even, op=ADD)
+            if n < SCALAR_ROUNDS:
+                nc.scalar.copy(out=to_quantise[n][:, 4:6, :], in_=sum2[n][:])
+            else:
+                nc.vector.tensor_tensor(
+                    out=to_quantise[n][:, 4:6, :].rearrange("p a (r u e) -> p (a r) u e", u=2, e=2),
+                    in0=odd, in1=even, op=ADD)
 
         def add_to_ten(n, first_slot, slots, piece):
             if first_slot % TEN == 0:
@@ -120,7 +126,8 @@ def tile_contractexpand_pa_t_e_kernel(tc, inputs_c_e, Ws_words, Ws_scales, bs, o
 
         def add_four(n):
             sum4[n] = fours.tile([P, D], F32, name="sum4")
-            nc.gpsimd.tensor_tensor(out=sum4[n][:], in0=sum2[n][:, 0, :], in1=sum2[n][:, 1, :], op=ADD)
+            engine = nc.vector if n == UNITS - 1 else nc.gpsimd
+            engine.tensor_tensor(out=sum4[n][:], in0=sum2[n][:, 0, :], in1=sum2[n][:, 1, :], op=ADD)
 
         def add_tens(n):
             first_slot = UNIT * n
@@ -146,13 +153,13 @@ def tile_contractexpand_pa_t_e_kernel(tc, inputs_c_e, Ws_words, Ws_scales, bs, o
                 quantise(n, 6, 7)
 
         def multiply_x(n):
-            acc = mps.tile([P, UNIT * P], F32, name="acc")
+            acc = acc_ps.tile([P, UNIT * P], F32, name="acc_x")
             product(acc[:], n, 0, 4, 0)
             hidden[n, 0] = acts.tile([P, UNIT * P], F32, name="hidden_x")
             bias_relu(hidden[n, 0][:], acc[:], 0)
 
         def multiply_sums(n):
-            acc = mps.tile([P, UNIT * P], F32, name="acc")
+            acc = acc_ps.tile([P, UNIT * P], F32, name="acc_sums")
             hidden[n, 1] = acts.tile([P, UNIT * P], F32, name="hidden_sums")
             product(acc[:, 0:2 * P], n, 4, 6, 1)
             product(acc[:, 2 * P:3 * P], n, 6, 7, 2)
@@ -169,7 +176,7 @@ def tile_contractexpand_pa_t_e_kernel(tc, inputs_c_e, Ws_words, Ws_scales, bs, o
             nc.sync.dma_start(out=rows, in_=copies.unsqueeze(1).to_broadcast([P, r // COPIES, COPIES * DO]))
 
         def back_x(n):
-            turned = bps.tile([P, UNIT, DO], F32, name="turned")
+            turned = turned_ps.tile([P, UNIT, DO], F32, name="turned_x")
             for a in range(UNIT):
                 nc.tensor.transpose(turned[:, 2 * (a % 2) + a // 2, :], hidden[n, 0][:, a * P:(a + 1) * P], ident[:])
             result_x = res.tile([P, UNIT, DO], F32, name="result_x")
@@ -178,7 +185,7 @@ def tile_contractexpand_pa_t_e_kernel(tc, inputs_c_e, Ws_words, Ws_scales, bs, o
 
         def back_sums(n):
             places = 4 if has_ten(n) else 3
-            turned = bps.tile([P, UNIT, DO], F32, name="turned")
+            turned = turned_ps.tile([P, UNIT, DO], F32, name="turned_sums")
             for a in range(places):
                 nc.tensor.transpose(turned[:, a, :], hidden[n, 1][:, a * P:(a + 1) * P], ident[:])
             result_sums = res.tile([P, UNIT, COPIES, DO], F32, name="result_sums")
@@ -218,7 +225,7 @@ def tile_contractexpand_pa_t_e_kernel(tc, inputs_c_e, Ws_words, Ws_scales, bs, o
         def prepare_bias(n):
             if n == 0:
                 nc.vector.tensor_copy(out=b_wide[:], in_=b_rows[:])
-                b_turned = bps.tile([P, UNIT, DO], F32, name="turned")
+                b_turned = turned_ps.tile([P, UNIT, DO], F32, name="turned_sums")
                 nc.tensor.transpose(b_turned[:, 0, :], b_wide[:], ident[:])
                 for s in range(NS):
                     nc.vector.tensor_scalar(out=bias_r[:, s:s + 1], in0=b_turned[:, 0, s:s + 1],

@@ -26,6 +26,7 @@ PLACES = 8
 COPIES = 2
 LOADS_AHEAD = 8
 SCALAR_ROUNDS = 2
+WARM_UP = 4
 LOADS_FIRST = 3
 FLOPS = 2 * D * DO * sum(N // r for r in GROUP)
 
@@ -184,24 +185,34 @@ def tile_contractexpand_pa_t_e_kernel(tc, inputs_c_e, Ws_words, Ws_scales, bs, o
             nc.sync.dma_start(out=out_slots[0][:, UNIT * n:UNIT * (n + 1), :], in_=result_x[:])
 
         def back_sums(n):
-            places = 4 if has_ten(n) else 3
             turned = turned_ps.tile([P, UNIT, DO], F32, name="turned_sums")
-            for a in range(places):
-                nc.tensor.transpose(turned[:, a, :], hidden[n, 1][:, a * P:(a + 1) * P], ident[:])
             result_sums = res.tile([P, UNIT, COPIES, DO], F32, name="result_sums")
-            nc.scalar.copy(out=result_sums[:, 0:places, :, :],
-                           in_=turned[:, 0:places, :].unsqueeze(2).to_broadcast([P, places, COPIES, DO]))
+
+            def copy_out(first, last):
+                nc.scalar.copy(out=result_sums[:, first:last, :, :],
+                               in_=turned[:, first:last, :].unsqueeze(2).to_broadcast([P, last - first, COPIES, DO]))
+
+            for a in ((3, 0, 1, 2) if has_ten(n) else (0, 1, 2)):
+                nc.tensor.transpose(turned[:, a, :], hidden[n, 1][:, a * P:(a + 1) * P], ident[:])
+            if has_ten(n):
+                copy_out(3, 4)
+                repeat_store(3, TEN * ((UNIT * n) // TEN), result_sums[:, 3, :, :].rearrange("p c d -> p (c d)"))
+            copy_out(0, 3)
             nc.sync.dma_start(out=out_slots[1][:, UNIT * n:UNIT * (n + 1), :],
                               in_=result_sums[:, 0:2, :, :].rearrange("p g c d -> p (g c) d"))
             repeat_store(2, UNIT * n, result_sums[:, 2, :, :].rearrange("p c d -> p (c d)"))
-            if has_ten(n):
-                repeat_store(3, TEN * ((UNIT * n) // TEN), result_sums[:, 3, :, :].rearrange("p c d -> p (c d)"))
 
         for n in range(LOADS_FIRST):
             load(n)
 
         ident = const.tile([P, P], F32, name="ident")
         make_identity(nc, ident[:])
+
+        zeros = const.tile([P, UNIT * P], BF16, name="zeros")
+        nc.vector.memset(zeros[:], 0.0)
+        idle_acc = acc_ps.tile([P, UNIT * P], F32, name="acc_x")
+        for again in range(WARM_UP):
+            nc.tensor.matmul(out=idle_acc[:], lhsT=zeros[:, 0:P], rhs=zeros[:], start=True, stop=True)
 
         w_codes = const.tile([P, NS, DO], U32, name="w_codes", align_bytes=64)
         nc.sync.dma_start(out=w_codes[:].bitcast(I32),

@@ -225,22 +225,18 @@ def tile_contractexpand_pa_t_e_kernel(tc, inputs_c_e, Ws_words, Ws_scales, bs, o
                 in_=Ws_scales[:, 4 * quadrant:4 * quadrant + 4, :].rearrange("s q o -> q s o").bitcast(I32),
             )
 
-        b_rows = const.tile([P, P], BF16, name="b_rows")
-        nc.vector.memset(b_rows[:], 0.0)
-        nc.sync.dma_start(out=b_rows[0:NS, :], in_=bs)
+        b_cols = const.tile([P, NS, 2], BF16, name="b_cols")
+        with nc.allow_non_contiguous_dma(reason="the biases, one value of each scale to a partition"):
+            nc.sync.dma_start(out=b_cols[:, :, 0:1], in_=bs.rearrange("s (o e) -> o s e", e=1))
         for n in range(LOADS_FIRST, LOADS_AHEAD):
             load(n)
-        b_wide = const.tile([P, P], F32, name="b_wide")
         bias_r = const.tile([P, NS], F32, name="bias_r")
 
         def prepare_bias(n):
             if n == 0:
-                nc.vector.tensor_copy(out=b_wide[:], in_=b_rows[:])
-                b_turned = turned_ps.tile([P, UNIT, DO], F32, name="turned_sums")
-                nc.tensor.transpose(b_turned[:, 0, :], b_wide[:], ident[:])
                 for s in range(NS):
-                    nc.vector.tensor_scalar(out=bias_r[:, s:s + 1], in0=b_turned[:, 0, s:s + 1],
-                                            scalar1=1.0 / GROUP[s], scalar2=None, op0=MULT)
+                    nc.gpsimd.tensor_scalar(out=bias_r[:, s:s + 1], in0=b_cols[:, s, 0:1],
+                                            scalar1=1.0 / GROUP[s], scalar2=0.0, op0=MULT, op1=ADD)
 
         def turn(stage, n):
             if 0 <= n < UNITS:

@@ -27,6 +27,7 @@ COPIES = 2
 LOADS_AHEAD = 8
 SCALAR_ROUNDS = 2
 WARM_UP = 4
+TEN_AHEAD = 2
 LOADS_FIRST = 3
 FLOPS = 2 * D * DO * sum(N // r for r in GROUP)
 
@@ -54,7 +55,7 @@ def tile_contractexpand_pa_t_e_kernel(tc, inputs_c_e, Ws_words, Ws_scales, bs, o
         sum2, sum4, running, hidden = {}, {}, {}, {}
 
         def has_ten(n):
-            return n % BLOCK_UNITS in (2, 4)
+            return (n + TEN_AHEAD) % BLOCK_UNITS in (2, 4) and n + TEN_AHEAD < UNITS
 
         def load(n):
             x_nat[n] = xin.tile([P, UNIT, D], BF16, name="x_nat")
@@ -119,7 +120,7 @@ def tile_contractexpand_pa_t_e_kernel(tc, inputs_c_e, Ws_words, Ws_scales, bs, o
             if first_slot % TEN == 0:
                 running["ten"] = piece
             elif (first_slot + slots) % TEN == 0:
-                nc.vector.tensor_tensor(out=to_quantise[n][:, 7, :], in0=running["ten"], in1=piece, op=ADD)
+                nc.vector.tensor_tensor(out=to_quantise[n - TEN_AHEAD][:, 7, :], in0=running["ten"], in1=piece, op=ADD)
             else:
                 partial = sums.tile([P, D], F32, name="partial")
                 nc.vector.tensor_tensor(out=partial[:], in0=running["ten"], in1=piece, op=ADD)
@@ -196,7 +197,8 @@ def tile_contractexpand_pa_t_e_kernel(tc, inputs_c_e, Ws_words, Ws_scales, bs, o
                 nc.tensor.transpose(turned[:, a, :], hidden[n, 1][:, a * P:(a + 1) * P], ident[:])
             if has_ten(n):
                 copy_out(3, 4)
-                repeat_store(3, TEN * ((UNIT * n) // TEN), result_sums[:, 3, :, :].rearrange("p c d -> p (c d)"))
+                repeat_store(3, TEN * ((UNIT * (n + TEN_AHEAD)) // TEN),
+                             result_sums[:, 3, :, :].rearrange("p c d -> p (c d)"))
             copy_out(0, 3)
             nc.sync.dma_start(out=out_slots[1][:, UNIT * n:UNIT * (n + 1), :],
                               in_=result_sums[:, 0:2, :, :].rearrange("p g c d -> p (g c) d"))

@@ -28,7 +28,7 @@ LOADS_AHEAD = 8
 SCALAR_ROUNDS = 2
 WARM_UP = 4
 TEN_AHEAD = 2
-LOADS_FIRST = 3
+LOADS_FIRST = 4
 FLOPS = 2 * D * DO * sum(N // r for r in GROUP)
 
 
@@ -38,7 +38,7 @@ def tile_contractexpand_pa_t_e_kernel(tc, inputs_c_e, Ws_words, Ws_scales, bs, o
     out_slots = out.rearrange("(s p t) d -> s p t d", s=NS, p=P)
 
     with tc.tile_pool(name="const", bufs=1) as const, \
-            tc.tile_pool(name="xin", bufs=LOADS_AHEAD + 2) as xin, \
+            tc.tile_pool(name="xin", bufs=LOADS_AHEAD // 2 + 2) as xin, \
             tc.tile_pool(name="bf", bufs=6) as bf, \
             tc.tile_pool(name="sums", bufs=3) as sums, \
             tc.tile_pool(name="fours", bufs=2) as fours, \
@@ -58,12 +58,16 @@ def tile_contractexpand_pa_t_e_kernel(tc, inputs_c_e, Ws_words, Ws_scales, bs, o
             return (n + TEN_AHEAD) % BLOCK_UNITS in (2, 4) and n + TEN_AHEAD < UNITS
 
         def load(n):
-            x_nat[n] = xin.tile([P, UNIT, D], BF16, name="x_nat")
+            if n % 2 == 1:
+                return
+            both = xin.tile([P, 2 * UNIT, D], BF16, name="x_nat")
+            x_nat[n], x_nat[n + 1] = both[:, 0:UNIT, :], both[:, UNIT:2 * UNIT, :]
             if n == 0:
                 for t in (0, 2, 1, 3):
-                    nc.sync.dma_start(out=x_nat[n][:, t, :], in_=x_slots[:, t, :])
+                    nc.sync.dma_start(out=both[:, t, :], in_=x_slots[:, t, :])
+                nc.sync.dma_start(out=both[:, UNIT:2 * UNIT, :], in_=x_slots[:, UNIT:2 * UNIT, :])
             else:
-                nc.sync.dma_start(out=x_nat[n][:], in_=x_slots[:, UNIT * n:UNIT * (n + 1), :])
+                nc.sync.dma_start(out=both[:], in_=x_slots[:, UNIT * n:UNIT * (n + 2), :])
 
         def quantise(n, first, last):
             nc.vector.quantize_mx(

@@ -9,6 +9,7 @@ U8 = mybir.dt.uint8
 FP8X4 = mybir.dt.float8_e4m3fn_x4
 ADD = mybir.AluOpType.add
 MULT = mybir.AluOpType.mult
+MAX = mybir.AluOpType.max
 RELU = mybir.ActivationFunctionType.Relu
 
 P = 128
@@ -25,9 +26,10 @@ TEN = GROUP[3]
 PLACES = 8
 COPIES = 2
 LOADS_AHEAD = 8
-SCALAR_ROUNDS = 2
+SCALAR_ROUNDS = 3
 WARM_UP = 4
 TEN_AHEAD = 2
+VECTOR_FINISHES = UNITS - 2
 LOADS_FIRST = 4
 FLOPS = 2 * D * DO * sum(N // r for r in GROUP)
 
@@ -52,7 +54,7 @@ def tile_contractexpand_pa_t_e_kernel(tc, inputs_c_e, Ws_words, Ws_scales, bs, o
             tc.manual_schedule():
 
         x_nat, transposed, to_quantise, codes, scales = {}, {}, {}, {}, {}
-        sum2, sum4, running, hidden = {}, {}, {}, {}
+        sum2, sum4, running, hidden, late = {}, {}, {}, {}, {}
 
         def has_ten(n):
             return (n + TEN_AHEAD) % BLOCK_UNITS in (2, 4) and n + TEN_AHEAD < UNITS
@@ -171,10 +173,30 @@ def tile_contractexpand_pa_t_e_kernel(tc, inputs_c_e, Ws_words, Ws_scales, bs, o
             product(acc[:, 2 * P:3 * P], n, 6, 7, 2)
             if has_ten(n):
                 product(acc[:, 3 * P:4 * P], n, 7, 8, 3)
+            if n == VECTOR_FINISHES:
+                late["acc"] = acc
+                return
             bias_relu(hidden[n, 1][:, 0:2 * P], acc[:, 0:2 * P], 1)
             bias_relu(hidden[n, 1][:, 2 * P:3 * P], acc[:, 2 * P:3 * P], 2)
             if has_ten(n):
                 bias_relu(hidden[n, 1][:, 3 * P:4 * P], acc[:, 3 * P:4 * P], 3)
+
+        def vector_bias(n):
+            if n == VECTOR_FINISHES:
+                for first, last, scale in ((0, 2 * P, 1), (2 * P, 3 * P, 2)):
+                    nc.vector.tensor_scalar(out=hidden[n, 1][:, first:last], in0=late["acc"][:, first:last],
+                                            scalar1=1.0 / GROUP[scale], scalar2=bias_r[:, scale:scale + 1],
+                                            op0=MULT, op1=ADD)
+
+        def vector_copy(n):
+            if n == VECTOR_FINISHES:
+                result_sums = res.tile([P, UNIT, COPIES, DO], F32, name="result_sums")
+                nc.vector.tensor_scalar(out=result_sums[:, 0:3, :, :],
+                                        in0=late["turned"][:, 0:3, :].unsqueeze(2).to_broadcast([P, 3, COPIES, DO]),
+                                        scalar1=0.0, scalar2=None, op0=MAX)
+                nc.sync.dma_start(out=out_slots[1][:, UNIT * n:UNIT * (n + 1), :],
+                                  in_=result_sums[:, 0:2, :, :].rearrange("p g c d -> p (g c) d"))
+                repeat_store(2, UNIT * n, result_sums[:, 2, :, :].rearrange("p c d -> p (c d)"))
 
         def repeat_store(scale, first_slot, copies):
             r = GROUP[scale]
@@ -191,6 +213,11 @@ def tile_contractexpand_pa_t_e_kernel(tc, inputs_c_e, Ws_words, Ws_scales, bs, o
 
         def back_sums(n):
             turned = turned_ps.tile([P, UNIT, DO], F32, name="turned_sums")
+            if n == VECTOR_FINISHES:
+                for a in range(3):
+                    nc.tensor.transpose(turned[:, a, :], hidden[n, 1][:, a * P:(a + 1) * P], ident[:])
+                late["turned"] = turned
+                return
             result_sums = res.tile([P, UNIT, COPIES, DO], F32, name="result_sums")
 
             def copy_out(first, last):
@@ -261,4 +288,6 @@ def tile_contractexpand_pa_t_e_kernel(tc, inputs_c_e, Ws_words, Ws_scales, bs, o
             turn(quantise_x, i - 1)
             turn(quantise_sums, i - 4)
             turn(round_four, i - 3)
+            turn(vector_bias, i - 5)
+            turn(vector_copy, i - 6)
             turn(add_four, i - 1)

@@ -29,7 +29,7 @@ LOADS_AHEAD = 8
 SCALAR_ROUNDS = 3
 WARM_UP = 4
 TEN_AHEAD = 2
-VECTOR_FINISHES = UNITS - 2
+VECTOR_FINISHES = (UNITS - 2, UNITS - 1)
 LOADS_FIRST = 4
 FLOPS = 2 * D * DO * sum(N // r for r in GROUP)
 
@@ -55,6 +55,13 @@ def tile_contractexpand_pa_t_e_kernel(tc, inputs_c_e, Ws_words, Ws_scales, bs, o
 
         x_nat, transposed, to_quantise, codes, scales = {}, {}, {}, {}, {}
         sum2, sum4, running, hidden, late = {}, {}, {}, {}, {}
+
+        now = {"turn": 0}
+
+        def bank(pool, shape, name, n):
+            if now["turn"] >= UNITS and n % 2 == 1:
+                return odd_ps.tile(shape, F32, name="xt")
+            return pool.tile(shape, F32, name=name)
 
         def has_ten(n):
             return (n + TEN_AHEAD) % BLOCK_UNITS in (2, 4) and n + TEN_AHEAD < UNITS
@@ -161,20 +168,20 @@ def tile_contractexpand_pa_t_e_kernel(tc, inputs_c_e, Ws_words, Ws_scales, bs, o
                 quantise(n, 6, 7)
 
         def multiply_x(n):
-            acc = acc_ps.tile([P, UNIT * P], F32, name="acc_x")
+            acc = bank(acc_ps, [P, UNIT * P], "acc_x", n)
             product(acc[:], n, 0, 4, 0)
             hidden[n, 0] = acts.tile([P, UNIT * P], F32, name="hidden_x")
             bias_relu(hidden[n, 0][:], acc[:], 0)
 
         def multiply_sums(n):
-            acc = acc_ps.tile([P, UNIT * P], F32, name="acc_sums")
+            acc = bank(acc_ps, [P, UNIT * P], "acc_sums", n)
             hidden[n, 1] = acts.tile([P, UNIT * P], F32, name="hidden_sums")
             product(acc[:, 0:2 * P], n, 4, 6, 1)
             product(acc[:, 2 * P:3 * P], n, 6, 7, 2)
             if has_ten(n):
                 product(acc[:, 3 * P:4 * P], n, 7, 8, 3)
-            if n == VECTOR_FINISHES:
-                late["acc"] = acc
+            if n in VECTOR_FINISHES:
+                late[n, "acc"] = acc
                 return
             bias_relu(hidden[n, 1][:, 0:2 * P], acc[:, 0:2 * P], 1)
             bias_relu(hidden[n, 1][:, 2 * P:3 * P], acc[:, 2 * P:3 * P], 2)
@@ -182,17 +189,17 @@ def tile_contractexpand_pa_t_e_kernel(tc, inputs_c_e, Ws_words, Ws_scales, bs, o
                 bias_relu(hidden[n, 1][:, 3 * P:4 * P], acc[:, 3 * P:4 * P], 3)
 
         def vector_bias(n):
-            if n == VECTOR_FINISHES:
+            if n in VECTOR_FINISHES:
                 for first, last, scale in ((0, 2 * P, 1), (2 * P, 3 * P, 2)):
-                    nc.vector.tensor_scalar(out=hidden[n, 1][:, first:last], in0=late["acc"][:, first:last],
+                    nc.vector.tensor_scalar(out=hidden[n, 1][:, first:last], in0=late[n, "acc"][:, first:last],
                                             scalar1=1.0 / GROUP[scale], scalar2=bias_r[:, scale:scale + 1],
                                             op0=MULT, op1=ADD)
 
         def vector_copy(n):
-            if n == VECTOR_FINISHES:
+            if n in VECTOR_FINISHES:
                 result_sums = res.tile([P, UNIT, COPIES, DO], F32, name="result_sums")
                 nc.vector.tensor_scalar(out=result_sums[:, 0:3, :, :],
-                                        in0=late["turned"][:, 0:3, :].unsqueeze(2).to_broadcast([P, 3, COPIES, DO]),
+                                        in0=late[n, "turned"][:, 0:3, :].unsqueeze(2).to_broadcast([P, 3, COPIES, DO]),
                                         scalar1=0.0, scalar2=None, op0=MAX)
                 nc.sync.dma_start(out=out_slots[1][:, UNIT * n:UNIT * (n + 1), :],
                                   in_=result_sums[:, 0:2, :, :].rearrange("p g c d -> p (g c) d"))
@@ -204,7 +211,7 @@ def tile_contractexpand_pa_t_e_kernel(tc, inputs_c_e, Ws_words, Ws_scales, bs, o
             nc.sync.dma_start(out=rows, in_=copies.unsqueeze(1).to_broadcast([P, r // COPIES, COPIES * DO]))
 
         def back_x(n):
-            turned = turned_ps.tile([P, UNIT, DO], F32, name="turned_x")
+            turned = bank(turned_ps, [P, UNIT, DO], "turned_x", n)
             for a in range(UNIT):
                 nc.tensor.transpose(turned[:, 2 * (a % 2) + a // 2, :], hidden[n, 0][:, a * P:(a + 1) * P], ident[:])
             result_x = res.tile([P, UNIT, DO], F32, name="result_x")
@@ -212,11 +219,11 @@ def tile_contractexpand_pa_t_e_kernel(tc, inputs_c_e, Ws_words, Ws_scales, bs, o
             nc.sync.dma_start(out=out_slots[0][:, UNIT * n:UNIT * (n + 1), :], in_=result_x[:])
 
         def back_sums(n):
-            turned = turned_ps.tile([P, UNIT, DO], F32, name="turned_sums")
-            if n == VECTOR_FINISHES:
+            turned = bank(turned_ps, [P, UNIT, DO], "turned_sums", n)
+            if n in VECTOR_FINISHES:
                 for a in range(3):
                     nc.tensor.transpose(turned[:, a, :], hidden[n, 1][:, a * P:(a + 1) * P], ident[:])
-                late["turned"] = turned
+                late[n, "turned"] = turned
                 return
             result_sums = res.tile([P, UNIT, COPIES, DO], F32, name="result_sums")
 
@@ -276,13 +283,23 @@ def tile_contractexpand_pa_t_e_kernel(tc, inputs_c_e, Ws_words, Ws_scales, bs, o
                 stage(n)
 
         for i in range(UNITS + 8):
+            now["turn"] = i
             turn(load, i + LOADS_AHEAD)
             turn(transpose, i)
             turn(prepare_bias, i - 2)
-            turn(back_x, i - 4)
-            turn(back_sums, i - 6)
-            turn(multiply_x, i - 3)
-            turn(multiply_sums, i - 5)
+            if i < UNITS:
+                turn(back_x, i - 4)
+                turn(back_sums, i - 6)
+                turn(multiply_x, i - 3)
+                turn(multiply_sums, i - 5)
+            else:
+                turn(multiply_x, i - 3)
+                if i - 5 in VECTOR_FINISHES:
+                    turn(multiply_sums, i - 5)
+                turn(back_x, i - 4)
+                turn(back_sums, i - 6)
+                if i - 5 not in VECTOR_FINISHES:
+                    turn(multiply_sums, i - 5)
             turn(add_pairs, i - 1)
             turn(add_tens, i - 2)
             turn(quantise_x, i - 1)

@@ -31,6 +31,9 @@ WARM_UP = 4
 TEN_AHEAD = 2
 VECTOR_FINISHES = (UNITS - 2, UNITS - 1)
 LOADS_FIRST = 4
+TAIL_FROM = 15
+TAIL_FOUR = 4
+TAIL_TEN = 5
 FLOPS = 2 * D * DO * sum(N // r for r in GROUP)
 
 
@@ -198,12 +201,16 @@ def tile_contractexpand_pa_t_e_kernel(tc, inputs_c_e, Ws_words, Ws_scales, bs, o
         def vector_copy(n):
             if n in VECTOR_FINISHES:
                 result_sums = res.tile([P, UNIT, COPIES, DO], F32, name="result_sums")
-                nc.vector.tensor_scalar(out=result_sums[:, 0:3, :, :],
-                                        in0=late[n, "turned"][:, 0:3, :].unsqueeze(2).to_broadcast([P, 3, COPIES, DO]),
+                nc.vector.tensor_scalar(out=result_sums[:, 0:2, :, :],
+                                        in0=late[n, "turned"][:, 0:2, :].unsqueeze(2).to_broadcast([P, 2, COPIES, DO]),
                                         scalar1=0.0, scalar2=None, op0=MAX)
                 nc.sync.dma_start(out=out_slots[1][:, UNIT * n:UNIT * (n + 1), :],
                                   in_=result_sums[:, 0:2, :, :].rearrange("p g c d -> p (g c) d"))
-                repeat_store(2, UNIT * n, result_sums[:, 2, :, :].rearrange("p c d -> p (c d)"))
+                wide_four = res.tile([P, TAIL_FOUR, DO], F32, name="wide_four")
+                nc.vector.tensor_scalar(out=wide_four[:], in0=late[n, "turned"][:, 2:3, :].to_broadcast([P, TAIL_FOUR, DO]),
+                                        scalar1=0.0, scalar2=None, op0=MAX)
+                nc.sync.dma_start(out=out_slots[2][:, UNIT * n:UNIT * (n + 1), :].rearrange("p (k c) d -> p k (c d)", c=TAIL_FOUR),
+                                  in_=wide_four[:].rearrange("p c d -> p (c d)").unsqueeze(1).to_broadcast([P, 4 // TAIL_FOUR, TAIL_FOUR * DO]))
 
         def repeat_store(scale, first_slot, copies):
             r = GROUP[scale]
@@ -233,6 +240,21 @@ def tile_contractexpand_pa_t_e_kernel(tc, inputs_c_e, Ws_words, Ws_scales, bs, o
 
             for a in ((3, 0, 1, 2) if has_ten(n) else (0, 1, 2)):
                 nc.tensor.transpose(turned[:, a, :], hidden[n, 1][:, a * P:(a + 1) * P], ident[:])
+            if n >= TAIL_FROM:
+                if has_ten(n):
+                    wide_ten = res.tile([P, TAIL_TEN, DO], F32, name="wide_ten")
+                    nc.scalar.copy(out=wide_ten[:], in_=turned[:, 3:4, :].to_broadcast([P, TAIL_TEN, DO]))
+                    first_slot = TEN * ((UNIT * (n + TEN_AHEAD)) // TEN)
+                    nc.sync.dma_start(out=out_slots[3][:, first_slot:first_slot + TEN, :].rearrange("p (k c) d -> p k (c d)", c=TAIL_TEN),
+                                      in_=wide_ten[:].rearrange("p c d -> p (c d)").unsqueeze(1).to_broadcast([P, TEN // TAIL_TEN, TAIL_TEN * DO]))
+                copy_out(0, 2)
+                nc.sync.dma_start(out=out_slots[1][:, UNIT * n:UNIT * (n + 1), :],
+                                  in_=result_sums[:, 0:2, :, :].rearrange("p g c d -> p (g c) d"))
+                wide_four = res.tile([P, TAIL_FOUR, DO], F32, name="wide_four")
+                nc.scalar.copy(out=wide_four[:], in_=turned[:, 2:3, :].to_broadcast([P, TAIL_FOUR, DO]))
+                nc.sync.dma_start(out=out_slots[2][:, UNIT * n:UNIT * (n + 1), :].rearrange("p (k c) d -> p k (c d)", c=TAIL_FOUR),
+                                  in_=wide_four[:].rearrange("p c d -> p (c d)").unsqueeze(1).to_broadcast([P, 4 // TAIL_FOUR, TAIL_FOUR * DO]))
+                return
             if has_ten(n):
                 copy_out(3, 4)
                 repeat_store(3, TEN * ((UNIT * (n + TEN_AHEAD)) // TEN),

@@ -31,6 +31,7 @@ WARM_UP = 4
 TEN_AHEAD = 2
 VECTOR_FINISHES = (UNITS - 2, UNITS - 1)
 LOADS_FIRST = 4
+ONE_FROM = 3
 TAIL_FROM = 15
 TAIL_FOUR = 4
 TAIL_TEN = 5
@@ -125,7 +126,7 @@ def tile_contractexpand_pa_t_e_kernel(tc, inputs_c_e, Ws_words, Ws_scales, bs, o
             even = to_quantise[n][:, 0:2, :].rearrange("p a (r u e) -> p (a r) u e", u=2, e=2)
             nc.vector.tensor_tensor(out=sum2[n][:].rearrange("p a (r u e) -> p (a r) u e", u=2, e=2),
                                     in0=odd, in1=even, op=ADD)
-            if n < SCALAR_ROUNDS:
+            if n < SCALAR_ROUNDS or (n < TAIL_FROM and n % BLOCK_UNITS == 1):
                 nc.scalar.copy(out=to_quantise[n][:, 4:6, :], in_=sum2[n][:])
             else:
                 nc.vector.tensor_tensor(
@@ -259,6 +260,14 @@ def tile_contractexpand_pa_t_e_kernel(tc, inputs_c_e, Ws_words, Ws_scales, bs, o
                 copy_out(3, 4)
                 repeat_store(3, TEN * ((UNIT * (n + TEN_AHEAD)) // TEN),
                              result_sums[:, 3, :, :].rearrange("p c d -> p (c d)"))
+            if ONE_FROM <= n < TAIL_FROM:
+                single = res.tile([P, 2, DO], F32, name="single")
+                nc.scalar.copy(out=single[:], in_=turned[:, 0:2, :])
+                for c in range(GROUP[1]):
+                    nc.sync.dma_start(out=out_slots[1][:, UNIT * n + c:UNIT * (n + 1):GROUP[1], :], in_=single[:])
+                copy_out(2, 3)
+                repeat_store(2, UNIT * n, result_sums[:, 2, :, :].rearrange("p c d -> p (c d)"))
+                return
             copy_out(0, 3)
             nc.sync.dma_start(out=out_slots[1][:, UNIT * n:UNIT * (n + 1), :],
                               in_=result_sums[:, 0:2, :, :].rearrange("p g c d -> p (g c) d"))

@@ -26,12 +26,12 @@ TEN = GROUP[3]
 PLACES = 8
 COPIES = 2
 LOADS_AHEAD = 8
-SCALAR_ROUNDS = 3
+SCALAR_ROUNDS = 4
 WARM_UP = 4
 TEN_AHEAD = 2
 VECTOR_FINISHES = (UNITS - 2, UNITS - 1)
 LOADS_FIRST = 4
-ONE_FROM = 3
+ONE_TO = 8
 TAIL_FROM = 15
 TAIL_FOUR = 4
 TAIL_TEN = 5
@@ -126,7 +126,7 @@ def tile_contractexpand_pa_t_e_kernel(tc, inputs_c_e, Ws_words, Ws_scales, bs, o
             even = to_quantise[n][:, 0:2, :].rearrange("p a (r u e) -> p (a r) u e", u=2, e=2)
             nc.vector.tensor_tensor(out=sum2[n][:].rearrange("p a (r u e) -> p (a r) u e", u=2, e=2),
                                     in0=odd, in1=even, op=ADD)
-            if n < SCALAR_ROUNDS or (n < TAIL_FROM and n % BLOCK_UNITS == 1):
+            if n < SCALAR_ROUNDS:
                 nc.scalar.copy(out=to_quantise[n][:, 4:6, :], in_=sum2[n][:])
             else:
                 nc.vector.tensor_tensor(
@@ -260,7 +260,7 @@ def tile_contractexpand_pa_t_e_kernel(tc, inputs_c_e, Ws_words, Ws_scales, bs, o
                 copy_out(3, 4)
                 repeat_store(3, TEN * ((UNIT * (n + TEN_AHEAD)) // TEN),
                              result_sums[:, 3, :, :].rearrange("p c d -> p (c d)"))
-            if ONE_FROM <= n < TAIL_FROM:
+            if n < ONE_TO:
                 single = res.tile([P, 2, DO], F32, name="single")
                 nc.scalar.copy(out=single[:], in_=turned[:, 0:2, :])
                 for c in range(GROUP[1]):
@@ -317,7 +317,7 @@ def tile_contractexpand_pa_t_e_kernel(tc, inputs_c_e, Ws_words, Ws_scales, bs, o
             now["turn"] = i
             turn(load, i + LOADS_AHEAD)
             turn(transpose, i)
-            turn(prepare_bias, i - 2)
+            turn(prepare_bias, i - 3)
             if i < UNITS:
                 turn(back_x, i - 4)
                 turn(back_sums, i - 6)

@@ -164,11 +164,14 @@ def tile_contractexpand_pa_t_e_kernel(tc, inputs_c_e, Ws_words, Ws_scales, bs, o
             scales[n] = mx.tile([P, PLACES, P], U8, name="scales", align_bytes=64)
             quantise(n, 0, 4)
 
-        def quantise_sums(n):
+        def quantise_twos(n):
+            if not has_ten(n):
+                quantise(n, 4, 6)
+
+        def quantise_rest(n):
             if has_ten(n):
                 quantise(n, 4, 8)
             else:
-                quantise(n, 4, 6)
                 quantise(n, 6, 7)
 
         def multiply_x(n):
@@ -334,8 +337,9 @@ def tile_contractexpand_pa_t_e_kernel(tc, inputs_c_e, Ws_words, Ws_scales, bs, o
             turn(add_pairs, i - 1)
             turn(add_tens, i - 2)
             turn(quantise_x, i - 1)
-            turn(quantise_sums, i - 4)
+            turn(quantise_twos, i - 4)
             turn(round_four, i - 3)
+            turn(quantise_rest, i - 4)
             turn(vector_bias, i - 5)
             turn(vector_copy, i - 6)
             turn(add_four, i - 1)

import concourse.mybir as mybir
from concourse.masks import make_identity

F32 = mybir.dt.float32
BF16 = mybir.dt.bfloat16
I32 = mybir.dt.int32
U32 = mybir.dt.uint32
U8 = mybir.dt.uint8
FP8X4 = mybir.dt.float8_e4m3fn_x4
ADD = mybir.AluOpType.add
MULT = mybir.AluOpType.mult
MAX = mybir.AluOpType.max
RELU = mybir.ActivationFunctionType.Relu

P = 128
N = 10240
D = 512
DO = 128
GROUP = (1, 2, 4, 10)
NS = len(GROUP)
SLOTS = N // P
UNIT = 4
UNITS = SLOTS // UNIT
BLOCK_UNITS = 5
TEN = GROUP[3]
PLACES = 8
COPIES = 2
LOADS_AHEAD = 8
SCALAR_ROUNDS = 4
WARM_UP = 4
TEN_AHEAD = 2
VECTOR_FINISHES = (UNITS - 2, UNITS - 1)
LOADS_FIRST = 4
ONE_TO = 8
TAIL_FROM = 15
TAIL_FOUR = 4
TAIL_TEN = 5
FLOPS = 2 * D * DO * sum(N // r for r in GROUP)


def tile_contractexpand_pa_t_e_kernel(tc, inputs_c_e, Ws_words, Ws_scales, bs, out):
    nc = tc.nc
    x_slots = inputs_c_e.rearrange("(p t) k -> p t k", p=P)
    out_slots = out.rearrange("(s p t) d -> s p t d", s=NS, p=P)

    with tc.tile_pool(name="const", bufs=1) as const, \
            tc.tile_pool(name="xin", bufs=LOADS_AHEAD // 2 + 2) as xin, \
            tc.tile_pool(name="bf", bufs=6) as bf, \
            tc.tile_pool(name="sums", bufs=3) as sums, \
            tc.tile_pool(name="fours", bufs=2) as fours, \
            tc.tile_pool(name="mx", bufs=7) as mx, \
            tc.tile_pool(name="acts", bufs=2) as acts, \
            tc.tile_pool(name="res", bufs=4) as res, \
            tc.psum_pool(name="even_ps", bufs=1) as even_ps, \
            tc.psum_pool(name="odd_ps", bufs=3) as odd_ps, \
            tc.psum_pool(name="acc_ps", bufs=1) as acc_ps, \
            tc.psum_pool(name="turned_ps", bufs=1) as turned_ps, \
            tc.manual_schedule():

        x_nat, transposed, to_quantise, codes, scales = {}, {}, {}, {}, {}
        sum2, sum4, running, hidden, late = {}, {}, {}, {}, {}

        now = {"turn": 0}

        def bank(pool, shape, name, n):
            if now["turn"] >= UNITS and n % 2 == 1:
                return odd_ps.tile(shape, F32, name="xt")
            return pool.tile(shape, F32, name=name)

        def has_ten(n):
            return (n + TEN_AHEAD) % BLOCK_UNITS in (2, 4) and n + TEN_AHEAD < UNITS

        def load(n):
            if n % 2 == 1:
                return
            both = xin.tile([P, 2 * UNIT, D], BF16, name="x_nat")
            x_nat[n], x_nat[n + 1] = both[:, 0:UNIT, :], both[:, UNIT:2 * UNIT, :]
            if n == 0:
                for t in (0, 2, 1, 3):
                    nc.sync.dma_start(out=both[:, t, :], in_=x_slots[:, t, :])
                nc.sync.dma_start(out=both[:, UNIT:2 * UNIT, :], in_=x_slots[:, UNIT:2 * UNIT, :])
            else:
                nc.sync.dma_start(out=both[:], in_=x_slots[:, UNIT * n:UNIT * (n + 2), :])

        def quantise(n, first, last):
            nc.vector.quantize_mx(
                out=codes[n][:, first:last, :].rearrange("p a c -> p (a c)").bitcast(FP8X4),
                scales=scales[n][:, first:last, :].rearrange("p a c -> p (a c)"),
                in_=to_quantise[n][:, first:last, :].rearrange("p a c -> p (a c)"),
            )

        def product(acc, n, first, last, scale):
            nc.tensor.matmul_mx(
                out=acc,
                lhsT=w_codes[:, scale, :].bitcast(FP8X4),
                lhsT_scale=w_scales[:, scale, :],
                rhs=codes[n][:, first:last, :].rearrange("p a c -> p (a c)").bitcast(FP8X4),
                rhs_scale=scales[n][:, first:last, :].rearrange("p a c -> p (a c)"),
                start=True,
                stop=True,
            )

        def bias_relu(target, acc, scale):
            nc.scalar.activation(out=target, in_=acc, func=RELU, bias=bias_r[:, scale:scale + 1],
                                 scale=1.0 / GROUP[scale])

        def transpose(n):
            to_quantise[n] = bf.tile([P, PLACES, D], BF16, name="to_quantise", align_bytes=64)
            for odd in range(2):
                xt = (odd_ps if odd else even_ps).tile([P, 2, 2, P], F32, name="xt")
                transposed[n, odd] = xt
                for pair in range(2):
                    words = x_nat[n][:, 2 * pair + odd, :].bitcast(F32)
                    for u in range(2):
                        nc.tensor.transpose(xt[:, u, pair, :], words[:, u:D // 2:2], ident[:])
                nc.scalar.copy(
                    out=to_quantise[n][:, 2 * odd:2 * odd + 2, :].rearrange("p a c -> p (a c)").bitcast(
                        F32).rearrange("p (x u) -> p x u", u=2),
                    in_=xt[:].rearrange("p u a r -> p (a r) u"),
                )

        def add_pairs(n):
            sum2[n] = sums.tile([P, 2, D], F32, name="sum2")
            odd = transposed[n, 1][:].rearrange("p u a r -> p u (a r)").bitcast(BF16).rearrange(
                "p u (x e) -> p x u e", e=2)
            even = to_quantise[n][:, 0:2, :].rearrange("p a (r u e) -> p (a r) u e", u=2, e=2)
            nc.vector.tensor_tensor(out=sum2[n][:].rearrange("p a (r u e) -> p (a r) u e", u=2, e=2),
                                    in0=odd, in1=even, op=ADD)
            if n < SCALAR_ROUNDS:
                nc.scalar.copy(out=to_quantise[n][:, 4:6, :], in_=sum2[n][:])
            else:
                nc.vector.tensor_tensor(
                    out=to_quantise[n][:, 4:6, :].rearrange("p a (r u e) -> p (a r) u e", u=2, e=2),
                    in0=odd, in1=even, op=ADD)

        def add_to_ten(n, first_slot, slots, piece):
            if first_slot % TEN == 0:
                running["ten"] = piece
            elif (first_slot + slots) % TEN == 0:
                nc.vector.tensor_tensor(out=to_quantise[n - TEN_AHEAD][:, 7, :], in0=running["ten"], in1=piece, op=ADD)
            else:
                partial = sums.tile([P, D], F32, name="partial")
                nc.vector.tensor_tensor(out=partial[:], in0=running["ten"], in1=piece, op=ADD)
                running["ten"] = partial[:]

        def add_four(n):
            sum4[n] = fours.tile([P, D], F32, name="sum4")
            engine = nc.vector if n == UNITS - 1 else nc.gpsimd
            engine.tensor_tensor(out=sum4[n][:], in0=sum2[n][:, 0, :], in1=sum2[n][:, 1, :], op=ADD)

        def add_tens(n):
            first_slot = UNIT * n
            if first_slot // TEN == (first_slot + UNIT - 1) // TEN:
                add_to_ten(n, first_slot, UNIT, sum4[n][:])
            else:
                add_to_ten(n, first_slot, 2, sum2[n][:, 0, :])
                add_to_ten(n, first_slot + 2, 2, sum2[n][:, 1, :])

        def round_four(n):
            nc.vector.tensor_copy(out=to_quantise[n][:, 6, :], in_=sum4[n][:])

        def quantise_x(n):
            codes[n] = mx.tile([P, PLACES, P], U32, name="codes", align_bytes=64)
            scales[n] = mx.tile([P, PLACES, P], U8, name="scales", align_bytes=64)
            quantise(n, 0, 4)

        def quantise_twos(n):
            if not has_ten(n):
                quantise(n, 4, 6)

        def quantise_rest(n):
            if has_ten(n):
                quantise(n, 4, 8)
            else:
                quantise(n, 6, 7)

        def multiply_x(n):
            acc = bank(acc_ps, [P, UNIT * P], "acc_x", n)
            product(acc[:], n, 0, 4, 0)
            hidden[n, 0] = acts.tile([P, UNIT * P], F32, name="hidden_x")
            bias_relu(hidden[n, 0][:], acc[:], 0)

        def multiply_sums(n):
            acc = bank(acc_ps, [P, UNIT * P], "acc_sums", n)
            hidden[n, 1] = acts.tile([P, UNIT * P], F32, name="hidden_sums")
            product(acc[:, 0:2 * P], n, 4, 6, 1)
            product(acc[:, 2 * P:3 * P], n, 6, 7, 2)
            if has_ten(n):
                product(acc[:, 3 * P:4 * P], n, 7, 8, 3)
            if n in VECTOR_FINISHES:
                late[n, "acc"] = acc
                return
            bias_relu(hidden[n, 1][:, 0:2 * P], acc[:, 0:2 * P], 1)
            bias_relu(hidden[n, 1][:, 2 * P:3 * P], acc[:, 2 * P:3 * P], 2)
            if has_ten(n):
                bias_relu(hidden[n, 1][:, 3 * P:4 * P], acc[:, 3 * P:4 * P], 3)

        def vector_bias(n):
            if n in VECTOR_FINISHES:
                for first, last, scale in ((0, 2 * P, 1), (2 * P, 3 * P, 2)):
                    nc.vector.tensor_scalar(out=hidden[n, 1][:, first:last], in0=late[n, "acc"][:, first:last],
                                            scalar1=1.0 / GROUP[scale], scalar2=bias_r[:, scale:scale + 1],
                                            op0=MULT, op1=ADD)

        def vector_copy(n):
            if n in VECTOR_FINISHES:
                result_sums = res.tile([P, UNIT, COPIES, DO], F32, name="result_sums")
                nc.vector.tensor_scalar(out=result_sums[:, 0:2, :, :],
                                        in0=late[n, "turned"][:, 0:2, :].unsqueeze(2).to_broadcast([P, 2, COPIES, DO]),
                                        scalar1=0.0, scalar2=None, op0=MAX)
                nc.sync.dma_start(out=out_slots[1][:, UNIT * n:UNIT * (n + 1), :],
                                  in_=result_sums[:, 0:2, :, :].rearrange("p g c d -> p (g c) d"))
                wide_four = res.tile([P, TAIL_FOUR, DO], F32, name="wide_four")
                nc.vector.tensor_scalar(out=wide_four[:], in0=late[n, "turned"][:, 2:3, :].to_broadcast([P, TAIL_FOUR, DO]),
                                        scalar1=0.0, scalar2=None, op0=MAX)
                nc.sync.dma_start(out=out_slots[2][:, UNIT * n:UNIT * (n + 1), :].rearrange("p (k c) d -> p k (c d)", c=TAIL_FOUR),
                                  in_=wide_four[:].rearrange("p c d -> p (c d)").unsqueeze(1).to_broadcast([P, 4 // TAIL_FOUR, TAIL_FOUR * DO]))

        def repeat_store(scale, first_slot, copies):
            r = GROUP[scale]
            rows = out_slots[scale][:, first_slot:first_slot + r, :].rearrange("p (k c) d -> p k (c d)", c=COPIES)
            nc.sync.dma_start(out=rows, in_=copies.unsqueeze(1).to_broadcast([P, r // COPIES, COPIES * DO]))

        def back_x(n):
            turned = bank(turned_ps, [P, UNIT, DO], "turned_x", n)
            for a in range(UNIT):
                nc.tensor.transpose(turned[:, 2 * (a % 2) + a // 2, :], hidden[n, 0][:, a * P:(a + 1) * P], ident[:])
            result_x = res.tile([P, UNIT, DO], F32, name="result_x")
            nc.scalar.copy(out=result_x[:], in_=turned[:])
            nc.sync.dma_start(out=out_slots[0][:, UNIT * n:UNIT * (n + 1), :], in_=result_x[:])

        def back_sums(n):
            turned = bank(turned_ps, [P, UNIT, DO], "turned_sums", n)
            if n in VECTOR_FINISHES:
                for a in range(3):
                    nc.tensor.transpose(turned[:, a, :], hidden[n, 1][:, a * P:(a + 1) * P], ident[:])
                late[n, "turned"] = turned
                return
            result_sums = res.tile([P, UNIT, COPIES, DO], F32, name="result_sums")

            def copy_out(first, last):
                nc.scalar.copy(out=result_sums[:, first:last, :, :],
                               in_=turned[:, first:last, :].unsqueeze(2).to_broadcast([P, last - first, COPIES, DO]))

            for a in ((3, 0, 1, 2) if has_ten(n) else (0, 1, 2)):
                nc.tensor.transpose(turned[:, a, :], hidden[n, 1][:, a * P:(a + 1) * P], ident[:])
            if n >= TAIL_FROM:
                if has_ten(n):
                    wide_ten = res.tile([P, TAIL_TEN, DO], F32, name="wide_ten")
                    nc.scalar.copy(out=wide_ten[:], in_=turned[:, 3:4, :].to_broadcast([P, TAIL_TEN, DO]))
                    first_slot = TEN * ((UNIT * (n + TEN_AHEAD)) // TEN)
                    nc.sync.dma_start(out=out_slots[3][:, first_slot:first_slot + TEN, :].rearrange("p (k c) d -> p k (c d)", c=TAIL_TEN),
                                      in_=wide_ten[:].rearrange("p c d -> p (c d)").unsqueeze(1).to_broadcast([P, TEN // TAIL_TEN, TAIL_TEN * DO]))
                copy_out(0, 2)
                nc.sync.dma_start(out=out_slots[1][:, UNIT * n:UNIT * (n + 1), :],
                                  in_=result_sums[:, 0:2, :, :].rearrange("p g c d -> p (g c) d"))
                wide_four = res.tile([P, TAIL_FOUR, DO], F32, name="wide_four")
                nc.scalar.copy(out=wide_four[:], in_=turned[:, 2:3, :].to_broadcast([P, TAIL_FOUR, DO]))
                nc.sync.dma_start(out=out_slots[2][:, UNIT * n:UNIT * (n + 1), :].rearrange("p (k c) d -> p k (c d)", c=TAIL_FOUR),
                                  in_=wide_four[:].rearrange("p c d -> p (c d)").unsqueeze(1).to_broadcast([P, 4 // TAIL_FOUR, TAIL_FOUR * DO]))
                return
            if has_ten(n):
                copy_out(3, 4)
                repeat_store(3, TEN * ((UNIT * (n + TEN_AHEAD)) // TEN),
                             result_sums[:, 3, :, :].rearrange("p c d -> p (c d)"))
            if n < ONE_TO:
                single = res.tile([P, 2, DO], F32, name="single")
                nc.scalar.copy(out=single[:], in_=turned[:, 0:2, :])
                for c in range(GROUP[1]):
                    nc.sync.dma_start(out=out_slots[1][:, UNIT * n + c:UNIT * (n + 1):GROUP[1], :], in_=single[:])
                copy_out(2, 3)
                repeat_store(2, UNIT * n, result_sums[:, 2, :, :].rearrange("p c d -> p (c d)"))
                return
            copy_out(0, 3)
            nc.sync.dma_start(out=out_slots[1][:, UNIT * n:UNIT * (n + 1), :],
                              in_=result_sums[:, 0:2, :, :].rearrange("p g c d -> p (g c) d"))
            repeat_store(2, UNIT * n, result_sums[:, 2, :, :].rearrange("p c d -> p (c d)"))

        for n in range(LOADS_FIRST):
            load(n)

        ident = const.tile([P, P], F32, name="ident")
        make_identity(nc, ident[:])

        zeros = const.tile([P, UNIT * P], BF16, name="zeros")
        nc.vector.memset(zeros[:], 0.0)
        idle_acc = acc_ps.tile([P, UNIT * P], F32, name="acc_x")
        for again in range(WARM_UP):
            nc.tensor.matmul(out=idle_acc[:], lhsT=zeros[:, 0:P], rhs=zeros[:], start=True, stop=True)

        w_codes = const.tile([P, NS, DO], U32, name="w_codes", align_bytes=64)
        nc.sync.dma_start(out=w_codes[:].bitcast(I32),
                          in_=Ws_words.rearrange("s p o t -> p s (o t)").bitcast(I32))
        w_scales = const.tile([P, NS, DO], U8, name="w_scales", align_bytes=64)
        nc.vector.memset(w_scales[:].bitcast(I32), 0)
        for quadrant in range(4):
            nc.sync.dma_start(
                out=w_scales[32 * quadrant:32 * quadrant + 4, :, :].bitcast(I32),
                in_=Ws_scales[:, 4 * quadrant:4 * quadrant + 4, :].rearrange("s q o -> q s o").bitcast(I32),
            )

        b_cols = const.tile([P, NS, 2], BF16, name="b_cols")
        with nc.allow_non_contiguous_dma(reason="the biases, one value of each scale to a partition"):
            nc.sync.dma_start(out=b_cols[:, :, 0:1], in_=bs.rearrange("s (o e) -> o s e", e=1))
        for n in range(LOADS_FIRST, LOADS_AHEAD):
            load(n)
        bias_r = const.tile([P, NS], F32, name="bias_r")

        def prepare_bias(n):
            if n == 0:
                for s in range(NS):
                    nc.gpsimd.tensor_scalar(out=bias_r[:, s:s + 1], in0=b_cols[:, s, 0:1],
                                            scalar1=1.0 / GROUP[s], scalar2=0.0, op0=MULT, op1=ADD)

        def turn(stage, n):
            if 0 <= n < UNITS:
                stage(n)

        for i in range(UNITS + 8):
            now["turn"] = i
            turn(load, i + LOADS_AHEAD)
            turn(transpose, i)
            turn(prepare_bias, i - 3)
            if i < UNITS:
                turn(back_x, i - 4)
                turn(back_sums, i - 6)
                turn(multiply_x, i - 3)
                turn(multiply_sums, i - 5)
            else:
                turn(multiply_x, i - 3)
                if i - 5 in VECTOR_FINISHES:
                    turn(multiply_sums, i - 5)
                turn(back_x, i - 4)
                turn(back_sums, i - 6)
                if i - 5 not in VECTOR_FINISHES:
                    turn(multiply_sums, i - 5)
            turn(add_pairs, i - 1)
            turn(add_tens, i - 2)
            turn(quantise_x, i - 1)
            turn(quantise_twos, i - 4)
            turn(round_four, i - 3)
            turn(quantise_rest, i - 4)
            turn(vector_bias, i - 5)
            turn(vector_copy, i - 6)
            turn(add_four, i - 1)
